import numpy as np
import ml_dtypes


def mxq(x, axis, fmt="e4m3"):
    dtype, down = {"e4m3": (ml_dtypes.float8_e4m3fn, 7), "e5m2": (ml_dtypes.float8_e5m2, 14)}[fmt]
    v = np.moveaxis(np.asarray(x, np.float32).astype(ml_dtypes.bfloat16).astype(np.float64), axis, -1)
    blocks = v.reshape(v.shape[:-1] + (-1, 32))
    amax = np.abs(blocks).max(-1, keepdims=True)
    byte = np.maximum(np.where(amax > 0, np.frexp(amax)[1] - 1 + 127, 0) - down, 1)
    scale = np.exp2(byte - 127.0)
    codes = (blocks / scale).astype(np.float32).astype(dtype).astype(np.float64)
    return np.moveaxis((codes * scale).reshape(v.shape), -1, axis)


WIDE = False


def mx_kscale(k):
    if not WIDE:
        return np.ones(k)
    levels = np.array([10, -10, 5, -5, 0])
    a = np.random.permutation(np.resize(levels, k // 512 * 4)).reshape(k // 512, 4)
    idx = np.arange(k)
    return np.exp2(a[idx // 512, idx % 128 // 32])


BF16 = ml_dtypes.bfloat16


def bf(x):
    return np.asarray(x, np.float32).astype(BF16)


def f64(x):
    return np.asarray(x).astype(np.float64)


E2M1 = np.array([0.0, 0.5, 1.0, 1.5, 2.0, 3.0, 4.0, 6.0, -0.0, -0.5, -1.0, -1.5, -2.0, -3.0, -4.0, -6.0])


def pack_weight(w, fmt):
    k, n = w.shape
    w = f64(bf(w)).reshape(k // 32, 32, n)
    amax = np.abs(w).max(1)
    if fmt == "e4m3":
        byte = np.frexp(amax)[1] - 1 + 127 - 7
    else:
        mant, ex = np.frexp(amax / 6.0)
        byte = np.where(mant > 0.5, ex, ex - 1) + 127
    byte = np.clip(np.where(amax > 0, byte, 1), 1, 254)
    scaled = (w * np.exp2(127.0 - byte)[:, None, :]).reshape(k, n).astype(np.float32)
    by_word = np.ascontiguousarray(scaled.reshape(k // 512, 128, 4, n).transpose(0, 1, 3, 2))
    if fmt == "e4m3":
        words = by_word.astype(ml_dtypes.float8_e4m3fn).view(np.uint8)
    else:
        c = by_word.astype(ml_dtypes.float4_e2m1fn).view(np.uint8) & 0xF
        words = c[..., 0::2] | (c[..., 1::2] << 4)
    return np.ascontiguousarray(words), np.ascontiguousarray(byte.astype(np.uint8).reshape(k // 512, 16, n))


def unpack_weight(words, scales, fmt):
    g, p, n, _ = words.shape
    if fmt == "e4m3":
        vals = np.ascontiguousarray(words).view(ml_dtypes.float8_e4m3fn).astype(np.float64)
    else:
        nib = np.empty((g, p, n, 4), np.uint8)
        nib[..., 0::2] = words & 0xF
        nib[..., 1::2] = words >> 4
        vals = E2M1[nib]
    vals = vals * np.repeat(np.exp2(scales.astype(np.float64) - 127.0), 8, axis=1)[..., None]
    return vals.transpose(0, 1, 3, 2).reshape(g * 512, n)


B, D, U1, U2 = 2048, 1024, 512, 256
THRESHOLD = 1.0


def setup_inputs():
    s, t = mx_kscale(D), mx_kscale(U1)
    c = s / s.mean()
    u = np.random.random(B)
    target = np.where(np.random.random(B) < 0.5, 0.5 + 0.35 * u, 1.15 + 0.45 * u)
    g = np.random.standard_normal((B, D)) * c
    x = g * (target / np.mean(np.abs(g), axis=1))[:, None]
    w1 = np.random.standard_normal((U1, D)) / np.sqrt(D) / c[None, :] * t[:, None]
    b1 = bf(np.random.standard_normal(U1) * 0.3 * t)
    w2 = np.random.standard_normal((U2, D)) / np.sqrt(D) / c[None, :] * t[:U2, None]
    b2 = bf(np.random.standard_normal(U2) * 0.3 * t[:U2])
    wf = np.random.standard_normal((D, U1)) * 1.5 / np.sqrt(U1) / t[None, :]
    bias_f = bf(np.random.standard_normal(D) * 0.3)
    W1_words, W1_scales = pack_weight(w1.T, "e4m3")
    W2_words, W2_scales = pack_weight(w2.T, "e4m3")
    Wf_words, Wf_scales = pack_weight(wf.T, "e4m3")
    return {"x": bf(x),
            "W1_words": W1_words,
            "W1_scales": W1_scales,
            "b1": b1,
            "W2_words": W2_words,
            "W2_scales": W2_scales,
            "b2": b2,
            "Wf_words": Wf_words,
            "Wf_scales": Wf_scales,
            "bf": bias_f}


def reference(x, W1_words, W1_scales, b1, W2_words, W2_scales, b2, Wf_words, Wf_scales, bf):
    x = f64(x)
    mask = np.mean(np.abs(x), axis=1) > THRESHOLD
    xq = mxq(x, 1, "e4m3")
    o1 = np.maximum((xq @ unpack_weight(W1_words, W1_scales, "e4m3")) + f64(b1), 0.0)
    o2 = np.maximum((xq @ unpack_weight(W2_words, W2_scales, "e4m3")) + f64(b2), 0.0)
    final_dim = W1_words.shape[2]
    o2p = np.pad(o2, ((0, 0), (0, final_dim - o2.shape[1])))
    branch_out = np.where(mask[:, None], o1, o2p)
    return (mxq(branch_out, 1, "e4m3") @ unpack_weight(Wf_words, Wf_scales, "e4m3")) + f64(bf)

@@ -1,0 +1,206 @@
+from contextlib import ExitStack
+
+import concourse.mybir as mybir
+from concourse.masks import make_identity
+
+F32 = mybir.dt.float32
+BF16 = mybir.dt.bfloat16
+I32 = mybir.dt.int32
+U32 = mybir.dt.uint32
+U8 = mybir.dt.uint8
+FP8X4 = mybir.dt.float8_e4m3fn_x4
+ALU = mybir.AluOpType
+ACT = mybir.ActivationFunctionType
+
+P = 128
+PACK = 4
+K_PASS = P * PACK
+BANK = 512
+
+ROWS, FEATURES, HIDDEN, HIDDEN2, OUT = 2048, 1024, 512, 256, 1024
+THRESHOLD = 1.0
+N_TILES = ROWS // P
+X_PASSES = FEATURES // K_PASS
+P2 = HIDDEN2 // PACK
+FAR = 1.0e38
+
+FLOPS = 2 * ROWS * FEATURES * (HIDDEN + HIDDEN2) + 2 * ROWS * HIDDEN * OUT
+
+
+def tile_dynamiclayer_kernel(
+    tc, x, W1_words, W1_scales, b1, W2_words, W2_scales, b2, Wf_words, Wf_scales, bf, out
+):
+    nc = tc.nc
+    x_rows = x.rearrange("(p i) k -> p i k", i=N_TILES)
+    out_rows = out.rearrange("(p i) n -> p i n", i=N_TILES)
+
+    with ExitStack() as ctx:
+        ctx.enter_context(tc.manual_schedule())
+        keep = ctx.enter_context(tc.tile_pool(name="keep", bufs=1))
+        work = ctx.enter_context(tc.tile_pool(name="work", bufs=3))
+        psum = ctx.enter_context(tc.psum_pool(name="psum", bufs=1))
+
+        x_sb = keep.tile([P, N_TILES, FEATURES], BF16)
+        w1_words = keep.tile([P, X_PASSES, HIDDEN], I32, align_bytes=64)
+        w2_words = keep.tile([P, X_PASSES, HIDDEN2], I32, align_bytes=64)
+        wf_words = keep.tile([P, 1, OUT], I32, align_bytes=64)
+        w1_scales = keep.tile([P, X_PASSES, HIDDEN], U8, align_bytes=64)
+        w2_scales = keep.tile([P, X_PASSES, HIDDEN2], U8, align_bytes=64)
+        wf_scales = keep.tile([P, 1, OUT], U8, align_bytes=64)
+        b1_all = keep.tile([P, HIDDEN], BF16)
+        b2_all = keep.tile([P, HIDDEN2], BF16)
+        bf_all = keep.tile([P, OUT], BF16)
+        ident_f32 = keep.tile([P, P], F32)
+        ident_bf16 = keep.tile([P, P], BF16)
+        abs_sum = keep.tile([P, N_TILES], F32)
+        push1 = keep.tile([P, N_TILES], F32)
+        push2 = keep.tile([P, N_TILES], F32)
+
+        def load_x(first, count):
+            nc.sync.dma_start(out=x_sb[:, first : first + count, :], in_=x_rows[:, first : first + count, :])
+
+        def load_weight(words_sb, scales_sb, words, scales):
+            nc.vector.memset(scales_sb[:].bitcast(I32), 0)
+            for quadrant in range(4):
+                nc.sync.dma_start(
+                    out=scales_sb[32 * quadrant : 32 * quadrant + 4].bitcast(I32),
+                    in_=scales[:, 4 * quadrant : 4 * quadrant + 4, :].rearrange("g r n -> r g n").bitcast(I32),
+                )
+            nc.sync.dma_start(out=words_sb[:], in_=words.rearrange("g p n t -> p g (n t)").bitcast(I32))
+
+        x_loads = []
+        first = 0
+        while first < N_TILES:
+            count = min(max(first, 1), 4)
+            x_loads.append((first, count))
+            first += count
+
+        load_x(*x_loads[0])
+        load_weight(w1_words, w1_scales, W1_words, W1_scales)
+        load_weight(w2_words, w2_scales, W2_words, W2_scales)
+        load_x(*x_loads[1])
+        load_x(*x_loads[2])
+        load_weight(wf_words, wf_scales, Wf_words, Wf_scales)
+        for first, count in x_loads[3:]:
+            load_x(first, count)
+
+        make_identity(nc, ident_f32[:])
+        nc.gpsimd.dma_start(out=b1_all[:], in_=b1.partition_broadcast(P))
+        nc.gpsimd.dma_start(out=b2_all[:], in_=b2.partition_broadcast(P))
+        make_identity(nc, ident_bf16[:])
+        nc.gpsimd.dma_start(out=bf_all[:], in_=bf.partition_broadcast(P))
+
+        x_grouped, x_codes, x_scales = {}, {}, {}
+        h_sorted, h_grouped, h_codes, h_scales = {}, {}, {}, {}
+
+        def transpose_x(i):
+            words = x_sb[:, i, :].bitcast(F32)
+            xt = psum.tile([P, X_PASSES, 2, P], F32, tag="xt", bufs=2)
+            for g in range(X_PASSES):
+                for u in range(2):
+                    nc.tensor.transpose(xt[:, g, u, :], words[:, 256 * g + u : 256 * (g + 1) : 2], ident_f32[:])
+            grouped = work.tile([P, FEATURES], BF16, tag="x_grouped", align_bytes=64)
+            nc.scalar.copy(
+                out=grouped[:].bitcast(F32).rearrange("p (g r u) -> p g r u", g=X_PASSES, u=2),
+                in_=xt[:].rearrange("p g u r -> p g r u"),
+            )
+            x_grouped[i] = grouped
+
+        def choose_branch(i):
+            magnitude = work.tile([P, FEATURES], BF16, tag="magnitude")
+            nc.scalar.activation(
+                out=magnitude[:], in_=x_sb[:, i, :], func=ACT.Abs, accum_out=abs_sum[:, i : i + 1]
+            )
+            nc.gpsimd.tensor_scalar(
+                out=push1[:, i : i + 1], in0=abs_sum[:, i : i + 1],
+                scalar1=THRESHOLD * FEATURES, scalar2=-FAR, op0=ALU.is_le, op1=ALU.mult,
+            )
+            nc.gpsimd.tensor_scalar(
+                out=push2[:, i : i + 1], in0=abs_sum[:, i : i + 1],
+                scalar1=THRESHOLD * FEATURES, scalar2=-FAR, op0=ALU.is_gt, op1=ALU.mult,
+            )
+
+        def quantise_x(i):
+            codes = work.tile([P, X_PASSES * P], U32, tag="x_codes", align_bytes=64)
+            scales = work.tile([P, X_PASSES * P], U8, tag="x_scales", align_bytes=64)
+            nc.vector.quantize_mx(out=codes[:].bitcast(FP8X4), scales=scales[:], in_=x_grouped[i][:])
+            x_codes[i], x_scales[i] = codes, scales
+
+        def first_layer(i):
+            acc1 = psum.tile([P, HIDDEN], F32, tag="acc1", bufs=2)
+            acc2 = psum.tile([P, HIDDEN2], F32, tag="acc2")
+            for acc, words_sb, scales_sb in ((acc1, w1_words, w1_scales), (acc2, w2_words, w2_scales)):
+                for g in range(X_PASSES):
+                    rows = slice(g * P, (g + 1) * P)
+                    nc.tensor.matmul_mx(
+                        out=acc[:],
+                        lhsT=x_codes[i][:, rows].bitcast(FP8X4),
+                        lhsT_scale=x_scales[i][:, rows],
+                        rhs=words_sb[:, g, :].bitcast(FP8X4),
+                        rhs_scale=scales_sb[:, g, :],
+                        start=(g == 0),
+                        stop=(g == X_PASSES - 1),
+                    )
+            sorted_h = work.tile([P, PACK, P], BF16, tag="h_sorted")
+            nc.vector.scalar_tensor_tensor(
+                out=sorted_h[:], in0=acc1[:].rearrange("r (p t) -> r t p", t=PACK), scalar=push1[:, i : i + 1],
+                in1=b1_all[:].rearrange("r (p t) -> r t p", t=PACK), op0=ALU.add, op1=ALU.add,
+            )
+            short = work.tile([P, PACK, P2], BF16, tag="short")
+            nc.vector.scalar_tensor_tensor(
+                out=short[:], in0=acc2[:].rearrange("r (p t) -> r t p", t=PACK), scalar=push2[:, i : i + 1],
+                in1=b2_all[:].rearrange("r (p t) -> r t p", t=PACK), op0=ALU.add, op1=ALU.add,
+            )
+            nc.vector.tensor_tensor(out=sorted_h[:, :, 0:P2], in0=sorted_h[:, :, 0:P2], in1=short[:], op=ALU.max)
+            h_sorted[i] = sorted_h
+
+        def transpose_h(i):
+            ht = psum.tile([P, PACK, P], BF16, tag="ht")
+            for t in range(PACK):
+                nc.tensor.transpose(ht[:, t, :], h_sorted[i][:, t, :], ident_bf16[:])
+            grouped = work.tile([P, P, PACK], BF16, tag="h_grouped", align_bytes=64)
+            nc.scalar.activation(out=grouped[:], in_=ht[:].rearrange("p t r -> p r t"), func=ACT.Relu)
+            h_grouped[i] = grouped
+
+        def quantise_h(i):
+            codes = work.tile([P, P], U32, tag="h_codes", align_bytes=64)
+            scales = work.tile([P, P], U8, tag="h_scales", align_bytes=64)
+            nc.vector.quantize_mx(
+                out=codes[:].bitcast(FP8X4), scales=scales[:], in_=h_grouped[i][:].rearrange("p r t -> p (r t)")
+            )
+            h_codes[i], h_scales[i] = codes, scales
+
+        def last_layer(i):
+            result = work.tile([P, OUT], F32, tag="result")
+            for first_col in range(0, OUT, BANK):
+                cols = slice(first_col, first_col + BANK)
+                acc = psum.tile([P, BANK], F32, tag="acc_out", bufs=2)
+                nc.tensor.matmul_mx(
+                    out=acc[:],
+                    lhsT=h_codes[i][:].bitcast(FP8X4),
+                    lhsT_scale=h_scales[i][:],
+                    rhs=wf_words[:, 0, cols].bitcast(FP8X4),
+                    rhs_scale=wf_scales[:, 0, cols],
+                    start=True,
+                    stop=True,
+                )
+                nc.vector.tensor_tensor(out=result[:, cols], in0=acc[:], in1=bf_all[:, cols], op=ALU.add)
+            nc.sync.dma_start(out=out_rows[:, i, :], in_=result[:])
+
+        def in_range(i):
+            return 0 <= i < N_TILES
+
+        for i in range(N_TILES + 3):
+            if in_range(i):
+                transpose_x(i)
+            if in_range(i - 2):
+                transpose_h(i - 2)
+            if in_range(i):
+                choose_branch(i)
+                quantise_x(i)
+            if in_range(i - 1):
+                first_layer(i - 1)
+            if in_range(i - 2):
+                quantise_h(i - 2)
+            if in_range(i - 3):
+                last_layer(i - 3)

@@ -35,7 +35,6 @@ def tile_dynamiclayer_kernel(
     out_rows = out.rearrange("(p i) n -> p i n", i=N_TILES)
 
     with ExitStack() as ctx:
-        ctx.enter_context(tc.manual_schedule())
         keep = ctx.enter_context(tc.tile_pool(name="keep", bufs=1))
         work = ctx.enter_context(tc.tile_pool(name="work", bufs=3))
         psum = ctx.enter_context(tc.psum_pool(name="psum", bufs=1))

@@ -16,10 +16,13 @@ P = 128
 PACK = 4
 K_PASS = P * PACK
 BANK = 512
+N_BANKS = 8
 
 ROWS, FEATURES, HIDDEN, HIDDEN2, OUT = 2048, 1024, 512, 256, 1024
 THRESHOLD = 1.0
 N_TILES = ROWS // P
+PAIR = 2
+N_PAIRS = N_TILES // PAIR
 X_PASSES = FEATURES // K_PASS
 P2 = HIDDEN2 // PACK
 FAR = 1.0e38
@@ -35,9 +38,10 @@ def tile_dynamiclayer_kernel(
     out_rows = out.rearrange("(p i) n -> p i n", i=N_TILES)
 
     with ExitStack() as ctx:
+        ctx.enter_context(tc.manual_schedule())
         keep = ctx.enter_context(tc.tile_pool(name="keep", bufs=1))
         work = ctx.enter_context(tc.tile_pool(name="work", bufs=3))
-        psum = ctx.enter_context(tc.psum_pool(name="psum", bufs=1))
+        psum = ctx.enter_context(tc.psum_pool(name="psum", bufs=N_BANKS))
 
         x_sb = keep.tile([P, N_TILES, FEATURES], BF16)
         w1_words = keep.tile([P, X_PASSES, HIDDEN], I32, align_bytes=64)
@@ -58,29 +62,33 @@ def tile_dynamiclayer_kernel(
         def load_x(first, count):
             nc.sync.dma_start(out=x_sb[:, first : first + count, :], in_=x_rows[:, first : first + count, :])
 
-        def load_weight(words_sb, scales_sb, words, scales):
+        def load_scales(scales_sb, scales):
             nc.vector.memset(scales_sb[:].bitcast(I32), 0)
             for quadrant in range(4):
                 nc.sync.dma_start(
                     out=scales_sb[32 * quadrant : 32 * quadrant + 4].bitcast(I32),
                     in_=scales[:, 4 * quadrant : 4 * quadrant + 4, :].rearrange("g r n -> r g n").bitcast(I32),
                 )
+
+        def load_words(words_sb, words):
             nc.sync.dma_start(out=words_sb[:], in_=words.rearrange("g p n t -> p g (n t)").bitcast(I32))
 
         x_loads = []
         first = 0
         while first < N_TILES:
-            count = min(max(first, 1), 4)
+            count = min(max(first, PAIR), 4)
             x_loads.append((first, count))
             first += count
 
         load_x(*x_loads[0])
-        load_weight(w1_words, w1_scales, W1_words, W1_scales)
-        load_weight(w2_words, w2_scales, W2_words, W2_scales)
+        load_scales(w1_scales, W1_scales)
+        load_words(w1_words, W1_words)
+        load_words(w2_words, W2_words)
+        load_scales(w2_scales, W2_scales)
         load_x(*x_loads[1])
-        load_x(*x_loads[2])
-        load_weight(wf_words, wf_scales, Wf_words, Wf_scales)
-        for first, count in x_loads[3:]:
+        load_scales(wf_scales, Wf_scales)
+        load_words(wf_words, Wf_words)
+        for first, count in x_loads[2:]:
             load_x(first, count)
 
         make_identity(nc, ident_f32[:])
@@ -92,114 +100,141 @@ def tile_dynamiclayer_kernel(
         x_grouped, x_codes, x_scales = {}, {}, {}
         h_sorted, h_grouped, h_codes, h_scales = {}, {}, {}, {}
 
-        def transpose_x(i):
-            words = x_sb[:, i, :].bitcast(F32)
-            xt = psum.tile([P, X_PASSES, 2, P], F32, tag="xt", bufs=2)
-            for g in range(X_PASSES):
-                for u in range(2):
-                    nc.tensor.transpose(xt[:, g, u, :], words[:, 256 * g + u : 256 * (g + 1) : 2], ident_f32[:])
-            grouped = work.tile([P, FEATURES], BF16, tag="x_grouped", align_bytes=64)
-            nc.scalar.copy(
-                out=grouped[:].bitcast(F32).rearrange("p (g r u) -> p g r u", g=X_PASSES, u=2),
-                in_=xt[:].rearrange("p g u r -> p g r u"),
-            )
-            x_grouped[i] = grouped
+        def transpose_x(pair):
+            grouped = work.tile([P, PAIR, FEATURES], BF16, tag="x_grouped", align_bytes=64)
+            banks = []
+            for s in range(PAIR):
+                words = x_sb[:, PAIR * pair + s, :].bitcast(F32)
+                xt = psum.tile([P, X_PASSES, 2, P], F32, tag="bank")
+                for g in range(X_PASSES):
+                    for u in range(2):
+                        nc.tensor.transpose(xt[:, g, u, :], words[:, 256 * g + u : 256 * (g + 1) : 2], ident_f32[:])
+                banks.append(xt)
+            for s in range(PAIR):
+                nc.scalar.copy(
+                    out=grouped[:, s, :].bitcast(F32).rearrange("p (g r u) -> p g r u", g=X_PASSES, u=2),
+                    in_=banks[s][:].rearrange("p g u r -> p g r u"),
+                )
+            x_grouped[pair] = grouped
 
-        def choose_branch(i):
-            magnitude = work.tile([P, FEATURES], BF16, tag="magnitude")
-            nc.scalar.activation(
-                out=magnitude[:], in_=x_sb[:, i, :], func=ACT.Abs, accum_out=abs_sum[:, i : i + 1]
-            )
+        def choose_branch(pair):
+            tiles = slice(PAIR * pair, PAIR * (pair + 1))
+            for i in range(PAIR * pair, PAIR * (pair + 1)):
+                magnitude = work.tile([P, FEATURES], BF16, tag="magnitude")
+                nc.scalar.activation(
+                    out=magnitude[:], in_=x_sb[:, i, :], func=ACT.Abs, accum_out=abs_sum[:, i : i + 1]
+                )
             nc.gpsimd.tensor_scalar(
-                out=push1[:, i : i + 1], in0=abs_sum[:, i : i + 1],
+                out=push1[:, tiles], in0=abs_sum[:, tiles],
                 scalar1=THRESHOLD * FEATURES, scalar2=-FAR, op0=ALU.is_le, op1=ALU.mult,
             )
             nc.gpsimd.tensor_scalar(
-                out=push2[:, i : i + 1], in0=abs_sum[:, i : i + 1],
+                out=push2[:, tiles], in0=abs_sum[:, tiles],
                 scalar1=THRESHOLD * FEATURES, scalar2=-FAR, op0=ALU.is_gt, op1=ALU.mult,
             )
 
-        def quantise_x(i):
-            codes = work.tile([P, X_PASSES * P], U32, tag="x_codes", align_bytes=64)
-            scales = work.tile([P, X_PASSES * P], U8, tag="x_scales", align_bytes=64)
-            nc.vector.quantize_mx(out=codes[:].bitcast(FP8X4), scales=scales[:], in_=x_grouped[i][:])
-            x_codes[i], x_scales[i] = codes, scales
+        def quantise_x(pair):
+            codes = work.tile([P, PAIR, X_PASSES, P], U32, tag="x_codes", align_bytes=64)
+            scales = work.tile([P, PAIR, X_PASSES, P], U8, tag="x_scales", align_bytes=64)
+            nc.vector.quantize_mx(
+                out=codes[:].rearrange("p s g r -> p (s g r)").bitcast(FP8X4),
+                scales=scales[:].rearrange("p s g r -> p (s g r)"),
+                in_=x_grouped[pair][:].rearrange("p s k -> p (s k)"),
+            )
+            x_codes[pair], x_scales[pair] = codes, scales
 
-        def first_layer(i):
-            acc1 = psum.tile([P, HIDDEN], F32, tag="acc1", bufs=2)
-            acc2 = psum.tile([P, HIDDEN2], F32, tag="acc2")
-            for acc, words_sb, scales_sb in ((acc1, w1_words, w1_scales), (acc2, w2_words, w2_scales)):
+        def first_layer(pair):
+            def passes(acc, s, words_sb, scales_sb):
                 for g in range(X_PASSES):
-                    rows = slice(g * P, (g + 1) * P)
                     nc.tensor.matmul_mx(
-                        out=acc[:],
-                        lhsT=x_codes[i][:, rows].bitcast(FP8X4),
-                        lhsT_scale=x_scales[i][:, rows],
+                        out=acc,
+                        lhsT=x_codes[pair][:, s, g, :].bitcast(FP8X4),
+                        lhsT_scale=x_scales[pair][:, s, g, :],
                         rhs=words_sb[:, g, :].bitcast(FP8X4),
                         rhs_scale=scales_sb[:, g, :],
                         start=(g == 0),
                         stop=(g == X_PASSES - 1),
                     )
-            sorted_h = work.tile([P, PACK, P], BF16, tag="h_sorted")
-            nc.vector.scalar_tensor_tensor(
-                out=sorted_h[:], in0=acc1[:].rearrange("r (p t) -> r t p", t=PACK), scalar=push1[:, i : i + 1],
-                in1=b1_all[:].rearrange("r (p t) -> r t p", t=PACK), op0=ALU.add, op1=ALU.add,
-            )
-            short = work.tile([P, PACK, P2], BF16, tag="short")
-            nc.vector.scalar_tensor_tensor(
-                out=short[:], in0=acc2[:].rearrange("r (p t) -> r t p", t=PACK), scalar=push2[:, i : i + 1],
-                in1=b2_all[:].rearrange("r (p t) -> r t p", t=PACK), op0=ALU.add, op1=ALU.add,
-            )
-            nc.vector.tensor_tensor(out=sorted_h[:, :, 0:P2], in0=sorted_h[:, :, 0:P2], in1=short[:], op=ALU.max)
-            h_sorted[i] = sorted_h
 
-        def transpose_h(i):
-            ht = psum.tile([P, PACK, P], BF16, tag="ht")
-            for t in range(PACK):
-                nc.tensor.transpose(ht[:, t, :], h_sorted[i][:, t, :], ident_bf16[:])
-            grouped = work.tile([P, P, PACK], BF16, tag="h_grouped", align_bytes=64)
-            nc.scalar.activation(out=grouped[:], in_=ht[:].rearrange("p t r -> p r t"), func=ACT.Relu)
-            h_grouped[i] = grouped
-
-        def quantise_h(i):
-            codes = work.tile([P, P], U32, tag="h_codes", align_bytes=64)
-            scales = work.tile([P, P], U8, tag="h_scales", align_bytes=64)
-            nc.vector.quantize_mx(
-                out=codes[:].bitcast(FP8X4), scales=scales[:], in_=h_grouped[i][:].rearrange("p r t -> p (r t)")
-            )
-            h_codes[i], h_scales[i] = codes, scales
-
-        def last_layer(i):
-            result = work.tile([P, OUT], F32, tag="result")
-            for first_col in range(0, OUT, BANK):
-                cols = slice(first_col, first_col + BANK)
-                acc = psum.tile([P, BANK], F32, tag="acc_out", bufs=2)
-                nc.tensor.matmul_mx(
-                    out=acc[:],
-                    lhsT=h_codes[i][:].bitcast(FP8X4),
-                    lhsT_scale=h_scales[i][:],
-                    rhs=wf_words[:, 0, cols].bitcast(FP8X4),
-                    rhs_scale=wf_scales[:, 0, cols],
-                    start=True,
-                    stop=True,
+            long_acc = []
+            for s in range(PAIR):
+                acc1 = psum.tile([P, HIDDEN], F32, tag="bank")
+                passes(acc1[:], s, w1_words, w1_scales)
+                long_acc.append(acc1)
+            acc2 = psum.tile([P, PAIR, HIDDEN2], F32, tag="bank")
+            for s in range(PAIR):
+                passes(acc2[:, s, :], s, w2_words, w2_scales)
+            sorted_h = work.tile([P, PAIR, PACK, P], BF16, tag="h_sorted")
+            short = work.tile([P, PAIR, PACK, P2], BF16, tag="short")
+            for s in range(PAIR):
+                i = PAIR * pair + s
+                nc.vector.scalar_tensor_tensor(
+                    out=sorted_h[:, s], in0=long_acc[s][:].rearrange("r (p t) -> r t p", t=PACK),
+                    scalar=push1[:, i : i + 1], in1=b1_all[:].rearrange("r (p t) -> r t p", t=PACK),
+                    op0=ALU.add, op1=ALU.add,
                 )
-                nc.vector.tensor_tensor(out=result[:, cols], in0=acc[:], in1=bf_all[:, cols], op=ALU.add)
-            nc.sync.dma_start(out=out_rows[:, i, :], in_=result[:])
+            for s in range(PAIR):
+                i = PAIR * pair + s
+                nc.vector.scalar_tensor_tensor(
+                    out=short[:, s], in0=acc2[:, s, :].rearrange("r (p t) -> r t p", t=PACK),
+                    scalar=push2[:, i : i + 1], in1=b2_all[:].rearrange("r (p t) -> r t p", t=PACK),
+                    op0=ALU.add, op1=ALU.add,
+                )
+            low = sorted_h[:].rearrange("r s t p -> r (s t) p")[:, :, 0:P2]
+            nc.vector.tensor_tensor(out=low, in0=low, in1=short[:].rearrange("r s t p -> r (s t) p"), op=ALU.max)
+            h_sorted[pair] = sorted_h
 
-        def in_range(i):
-            return 0 <= i < N_TILES
+        def transpose_h(pair):
+            ht = psum.tile([P, PAIR, PACK, P], BF16, tag="bank")
+            for s in range(PAIR):
+                for t in range(PACK):
+                    nc.tensor.transpose(ht[:, s, t, :], h_sorted[pair][:, s, t, :], ident_bf16[:])
+            grouped = work.tile([P, PAIR, P, PACK], BF16, tag="h_grouped", align_bytes=64)
+            nc.scalar.activation(out=grouped[:], in_=ht[:].rearrange("p s t r -> p s r t"), func=ACT.Relu)
+            h_grouped[pair] = grouped
 
-        for i in range(N_TILES + 3):
-            if in_range(i):
-                transpose_x(i)
-            if in_range(i - 2):
-                transpose_h(i - 2)
-            if in_range(i):
-                choose_branch(i)
-                quantise_x(i)
-            if in_range(i - 1):
-                first_layer(i - 1)
-            if in_range(i - 2):
-                quantise_h(i - 2)
-            if in_range(i - 3):
-                last_layer(i - 3)
+        def quantise_h(pair):
+            codes = work.tile([P, PAIR, P], U32, tag="h_codes", align_bytes=64)
+            scales = work.tile([P, PAIR, P], U8, tag="h_scales", align_bytes=64)
+            nc.vector.quantize_mx(
+                out=codes[:].rearrange("p s r -> p (s r)").bitcast(FP8X4),
+                scales=scales[:].rearrange("p s r -> p (s r)"),
+                in_=h_grouped[pair][:].rearrange("p s r t -> p (s r t)"),
+            )
+            h_codes[pair], h_scales[pair] = codes, scales
+
+        def last_layer(pair):
+            for s in range(PAIR):
+                result = work.tile([P, OUT], F32, tag="result")
+                for first_col in range(0, OUT, BANK):
+                    cols = slice(first_col, first_col + BANK)
+                    acc = psum.tile([P, BANK], F32, tag="bank")
+                    nc.tensor.matmul_mx(
+                        out=acc[:],
+                        lhsT=h_codes[pair][:, s, :].bitcast(FP8X4),
+                        lhsT_scale=h_scales[pair][:, s, :],
+                        rhs=wf_words[:, 0, cols].bitcast(FP8X4),
+                        rhs_scale=wf_scales[:, 0, cols],
+                        start=True,
+                        stop=True,
+                    )
+                    nc.vector.tensor_tensor(out=result[:, cols], in0=acc[:], in1=bf_all[:, cols], op=ALU.add)
+                nc.sync.dma_start(out=out_rows[:, PAIR * pair + s, :], in_=result[:])
+
+        def in_range(pair):
+            return 0 <= pair < N_PAIRS
+
+        for j in range(N_PAIRS + 3):
+            if in_range(j):
+                transpose_x(j)
+            if in_range(j - 2):
+                transpose_h(j - 2)
+            if in_range(j):
+                choose_branch(j)
+                quantise_x(j)
+            if in_range(j - 1):
+                first_layer(j - 1)
+            if in_range(j - 2):
+                quantise_h(j - 2)
+            if in_range(j - 3):
+                last_layer(j - 3)

@@ -55,9 +55,6 @@ def tile_dynamiclayer_kernel(
         bf_all = keep.tile([P, OUT], BF16)
         ident_f32 = keep.tile([P, P], F32)
         ident_bf16 = keep.tile([P, P], BF16)
-        abs_sum = keep.tile([P, N_TILES], F32)
-        push1 = keep.tile([P, N_TILES], F32)
-        push2 = keep.tile([P, N_TILES], F32)
 
         def load_x(first, count):
             nc.sync.dma_start(out=x_sb[:, first : first + count, :], in_=x_rows[:, first : first + count, :])
@@ -76,19 +73,20 @@ def tile_dynamiclayer_kernel(
         x_loads = []
         first = 0
         while first < N_TILES:
-            count = min(max(first, PAIR), 4)
+            count = min(max(first, 1), 4)
             x_loads.append((first, count))
             first += count
 
         load_x(*x_loads[0])
+        load_x(*x_loads[1])
         load_scales(w1_scales, W1_scales)
         load_words(w1_words, W1_words)
         load_words(w2_words, W2_words)
         load_scales(w2_scales, W2_scales)
-        load_x(*x_loads[1])
+        load_x(*x_loads[2])
         load_scales(wf_scales, Wf_scales)
         load_words(wf_words, Wf_words)
-        for first, count in x_loads[2:]:
+        for first, count in x_loads[3:]:
             load_x(first, count)
 
         make_identity(nc, ident_f32[:])
@@ -99,6 +97,7 @@ def tile_dynamiclayer_kernel(
 
         x_grouped, x_codes, x_scales = {}, {}, {}
         h_sorted, h_grouped, h_codes, h_scales = {}, {}, {}, {}
+        push1, push2 = {}, {}
 
         def transpose_x(pair):
             grouped = work.tile([P, PAIR, FEATURES], BF16, tag="x_grouped", align_bytes=64)
@@ -118,20 +117,20 @@ def tile_dynamiclayer_kernel(
             x_grouped[pair] = grouped
 
         def choose_branch(pair):
-            tiles = slice(PAIR * pair, PAIR * (pair + 1))
-            for i in range(PAIR * pair, PAIR * (pair + 1)):
+            abs_sum = work.tile([P, PAIR], F32, tag="abs_sum")
+            for s in range(PAIR):
                 magnitude = work.tile([P, FEATURES], BF16, tag="magnitude")
                 nc.scalar.activation(
-                    out=magnitude[:], in_=x_sb[:, i, :], func=ACT.Abs, accum_out=abs_sum[:, i : i + 1]
+                    out=magnitude[:], in_=x_sb[:, PAIR * pair + s, :], func=ACT.Abs, accum_out=abs_sum[:, s : s + 1]
                 )
-            nc.gpsimd.tensor_scalar(
-                out=push1[:, tiles], in0=abs_sum[:, tiles],
-                scalar1=THRESHOLD * FEATURES, scalar2=-FAR, op0=ALU.is_le, op1=ALU.mult,
-            )
-            nc.gpsimd.tensor_scalar(
-                out=push2[:, tiles], in0=abs_sum[:, tiles],
-                scalar1=THRESHOLD * FEATURES, scalar2=-FAR, op0=ALU.is_gt, op1=ALU.mult,
-            )
+            to_long = work.tile([P, PAIR], F32, tag="to_long")
+            to_short = work.tile([P, PAIR], F32, tag="to_short")
+            for push, switched_off in ((to_long, ALU.is_le), (to_short, ALU.is_gt)):
+                nc.gpsimd.tensor_scalar(
+                    out=push[:], in0=abs_sum[:], scalar1=THRESHOLD * FEATURES, scalar2=-FAR,
+                    op0=switched_off, op1=ALU.mult,
+                )
+            push1[pair], push2[pair] = to_long, to_short
 
         def quantise_x(pair):
             codes = work.tile([P, PAIR, X_PASSES, P], U32, tag="x_codes", align_bytes=64)
@@ -167,17 +166,15 @@ def tile_dynamiclayer_kernel(
             sorted_h = work.tile([P, PAIR, PACK, P], BF16, tag="h_sorted")
             short = work.tile([P, PAIR, PACK, P2], BF16, tag="short")
             for s in range(PAIR):
-                i = PAIR * pair + s
                 nc.vector.scalar_tensor_tensor(
                     out=sorted_h[:, s], in0=long_acc[s][:].rearrange("r (p t) -> r t p", t=PACK),
-                    scalar=push1[:, i : i + 1], in1=b1_all[:].rearrange("r (p t) -> r t p", t=PACK),
+                    scalar=push1[pair][:, s : s + 1], in1=b1_all[:].rearrange("r (p t) -> r t p", t=PACK),
                     op0=ALU.add, op1=ALU.add,
                 )
             for s in range(PAIR):
-                i = PAIR * pair + s
                 nc.vector.scalar_tensor_tensor(
                     out=short[:, s], in0=acc2[:, s, :].rearrange("r (p t) -> r t p", t=PACK),
-                    scalar=push2[:, i : i + 1], in1=b2_all[:].rearrange("r (p t) -> r t p", t=PACK),
+                    scalar=push2[pair][:, s : s + 1], in1=b2_all[:].rearrange("r (p t) -> r t p", t=PACK),
                     op0=ALU.add, op1=ALU.add,
                 )
             low = sorted_h[:].rearrange("r s t p -> r (s t) p")[:, :, 0:P2]
@@ -205,7 +202,7 @@ def tile_dynamiclayer_kernel(
 
         def last_layer(pair):
             for s in range(PAIR):
-                result = work.tile([P, OUT], F32, tag="result")
+                result = work.tile([P, OUT], F32, tag="result", bufs=4)
                 for first_col in range(0, OUT, BANK):
                     cols = slice(first_col, first_col + BANK)
                     acc = psum.tile([P, BANK], F32, tag="bank")
@@ -218,7 +215,13 @@ def tile_dynamiclayer_kernel(
                         start=True,
                         stop=True,
                     )
-                    nc.vector.tensor_tensor(out=result[:, cols], in0=acc[:], in1=bf_all[:, cols], op=ALU.add)
+                    if s == 0 and first_col == BANK:
+                        nc.scalar.copy(out=result[:, cols], in_=acc[:])
+                        nc.gpsimd.tensor_tensor(
+                            out=result[:, cols], in0=result[:, cols], in1=bf_all[:, cols], op=ALU.add
+                        )
+                    else:
+                        nc.vector.tensor_tensor(out=result[:, cols], in0=acc[:], in1=bf_all[:, cols], op=ALU.add)
                 nc.sync.dma_start(out=out_rows[:, PAIR * pair + s, :], in_=result[:])
 
         def in_range(pair):
@@ -231,9 +234,10 @@ def tile_dynamiclayer_kernel(
                 transpose_h(j - 2)
             if in_range(j):
                 choose_branch(j)
-                quantise_x(j)
             if in_range(j - 1):
                 first_layer(j - 1)
+            if in_range(j):
+                quantise_x(j)
             if in_range(j - 2):
                 quantise_h(j - 2)
             if in_range(j - 3):

@@ -50,9 +50,11 @@ def tile_dynamiclayer_kernel(
         w1_scales = keep.tile([P, X_PASSES, HIDDEN], U8, align_bytes=64)
         w2_scales = keep.tile([P, X_PASSES, HIDDEN2], U8, align_bytes=64)
         wf_scales = keep.tile([P, 1, OUT], U8, align_bytes=64)
-        b1_all = keep.tile([P, HIDDEN], BF16)
-        b2_all = keep.tile([P, HIDDEN2], BF16)
-        bf_all = keep.tile([P, OUT], BF16)
+        bias_rows = keep.tile([P, HIDDEN + HIDDEN2 + OUT], BF16)
+        ones = keep.tile([P, P], BF16)
+        b1_sorted = keep.tile([P, PACK, P], F32)
+        b2_sorted = keep.tile([P, PACK, P2], F32)
+        bf_all = keep.tile([P, OUT], F32)
         ident_f32 = keep.tile([P, P], F32)
         ident_bf16 = keep.tile([P, P], BF16)
 
@@ -77,6 +79,9 @@ def tile_dynamiclayer_kernel(
             x_loads.append((first, count))
             first += count
 
+        nc.vector.memset(bias_rows[:].bitcast(I32), 0)
+        nc.vector.memset(ones[:], 1.0)
+
         load_x(*x_loads[0])
         load_x(*x_loads[1])
         load_scales(w1_scales, W1_scales)
@@ -90,10 +95,29 @@ def tile_dynamiclayer_kernel(
             load_x(first, count)
 
         make_identity(nc, ident_f32[:])
-        nc.gpsimd.dma_start(out=b1_all[:], in_=b1.partition_broadcast(P))
-        nc.gpsimd.dma_start(out=b2_all[:], in_=b2.partition_broadcast(P))
+        first = 0
+        for bias in (b1, b2, bf):
+            nc.gpsimd.dma_start(out=bias_rows[0:1, first : first + bias.shape[0]], in_=bias.unsqueeze(0))
+            first += bias.shape[0]
         make_identity(nc, ident_bf16[:])
-        nc.gpsimd.dma_start(out=bf_all[:], in_=bf.partition_broadcast(P))
+
+        def spread_bias(first_col, width):
+            bank = psum.tile([P, width], F32, tag="bank")
+            nc.tensor.matmul(
+                out=bank[:], lhsT=ones[:], rhs=bias_rows[:, first_col : first_col + width], start=True, stop=True
+            )
+            return bank
+
+        def spread_first_biases():
+            b1_bank = spread_bias(0, HIDDEN)
+            nc.vector.tensor_copy(out=b1_sorted[:], in_=b1_bank[:].rearrange("r (p t) -> r t p", t=PACK))
+            b2_bank = spread_bias(HIDDEN, HIDDEN2)
+            nc.vector.tensor_copy(out=b2_sorted[:], in_=b2_bank[:].rearrange("r (p t) -> r t p", t=PACK))
+
+        def spread_last_bias():
+            for first_col in range(0, OUT, BANK):
+                bf_bank = spread_bias(HIDDEN + HIDDEN2 + first_col, BANK)
+                nc.vector.tensor_copy(out=bf_all[:, first_col : first_col + BANK], in_=bf_bank[:])
 
         x_grouped, x_codes, x_scales = {}, {}, {}
         h_sorted, h_grouped, h_codes, h_scales = {}, {}, {}, {}
@@ -168,13 +192,13 @@ def tile_dynamiclayer_kernel(
             for s in range(PAIR):
                 nc.vector.scalar_tensor_tensor(
                     out=sorted_h[:, s], in0=long_acc[s][:].rearrange("r (p t) -> r t p", t=PACK),
-                    scalar=push1[pair][:, s : s + 1], in1=b1_all[:].rearrange("r (p t) -> r t p", t=PACK),
+                    scalar=push1[pair][:, s : s + 1], in1=b1_sorted[:],
                     op0=ALU.add, op1=ALU.add,
                 )
             for s in range(PAIR):
                 nc.vector.scalar_tensor_tensor(
                     out=short[:, s], in0=acc2[:, s, :].rearrange("r (p t) -> r t p", t=PACK),
-                    scalar=push2[pair][:, s : s + 1], in1=b2_all[:].rearrange("r (p t) -> r t p", t=PACK),
+                    scalar=push2[pair][:, s : s + 1], in1=b2_sorted[:],
                     op0=ALU.add, op1=ALU.add,
                 )
             low = sorted_h[:].rearrange("r s t p -> r (s t) p")[:, :, 0:P2]
@@ -222,7 +246,7 @@ def tile_dynamiclayer_kernel(
                         )
                     else:
                         nc.vector.tensor_tensor(out=result[:, cols], in0=acc[:], in1=bf_all[:, cols], op=ALU.add)
-                nc.sync.dma_start(out=out_rows[:, PAIR * pair + s, :], in_=result[:])
+                    nc.sync.dma_start(out=out_rows[:, PAIR * pair + s, cols], in_=result[:, cols])
 
         def in_range(pair):
             return 0 <= pair < N_PAIRS
@@ -238,6 +262,10 @@ def tile_dynamiclayer_kernel(
                 first_layer(j - 1)
             if in_range(j):
                 quantise_x(j)
+            if j == 0:
+                spread_first_biases()
+            if j == 1:
+                spread_last_bias()
             if in_range(j - 2):
                 quantise_h(j - 2)
             if in_range(j - 3):

@@ -21,8 +21,8 @@ N_BANKS = 8
 ROWS, FEATURES, HIDDEN, HIDDEN2, OUT = 2048, 1024, 512, 256, 1024
 THRESHOLD = 1.0
 N_TILES = ROWS // P
-PAIR = 2
-N_PAIRS = N_TILES // PAIR
+GROUPS = [(first, 2) for first in range(0, N_TILES - 2, 2)] + [(N_TILES - 2, 1), (N_TILES - 1, 1)]
+N_GROUPS = len(GROUPS)
 X_PASSES = FEATURES // K_PASS
 P2 = HIDDEN2 // PACK
 FAR = 1.0e38
@@ -123,56 +123,61 @@ def tile_dynamiclayer_kernel(
         h_sorted, h_grouped, h_codes, h_scales = {}, {}, {}, {}
         push1, push2 = {}, {}
 
-        def transpose_x(pair):
-            grouped = work.tile([P, PAIR, FEATURES], BF16, tag="x_grouped", align_bytes=64)
+        def transpose_x(group):
+            first_tile, count = GROUPS[group]
+            grouped = work.tile([P, count, FEATURES], BF16, tag="x_grouped", align_bytes=64)
             banks = []
-            for s in range(PAIR):
-                words = x_sb[:, PAIR * pair + s, :].bitcast(F32)
+            for s in range(count):
+                words = x_sb[:, first_tile + s, :].bitcast(F32)
                 xt = psum.tile([P, X_PASSES, 2, P], F32, tag="bank")
                 for g in range(X_PASSES):
                     for u in range(2):
                         nc.tensor.transpose(xt[:, g, u, :], words[:, 256 * g + u : 256 * (g + 1) : 2], ident_f32[:])
                 banks.append(xt)
-            for s in range(PAIR):
+            for s in range(count):
                 nc.scalar.copy(
                     out=grouped[:, s, :].bitcast(F32).rearrange("p (g r u) -> p g r u", g=X_PASSES, u=2),
                     in_=banks[s][:].rearrange("p g u r -> p g r u"),
                 )
-            x_grouped[pair] = grouped
+            x_grouped[group] = grouped
 
-        def choose_branch(pair):
-            abs_sum = work.tile([P, PAIR], F32, tag="abs_sum")
-            for s in range(PAIR):
+        def choose_branch(group):
+            first_tile, count = GROUPS[group]
+            abs_sum = work.tile([P, count], F32, tag="abs_sum")
+            for s in range(count):
                 magnitude = work.tile([P, FEATURES], BF16, tag="magnitude")
                 nc.scalar.activation(
-                    out=magnitude[:], in_=x_sb[:, PAIR * pair + s, :], func=ACT.Abs, accum_out=abs_sum[:, s : s + 1]
+                    out=magnitude[:], in_=x_sb[:, first_tile + s, :], func=ACT.Abs, accum_out=abs_sum[:, s : s + 1]
                 )
-            to_long = work.tile([P, PAIR], F32, tag="to_long")
-            to_short = work.tile([P, PAIR], F32, tag="to_short")
+            to_long = work.tile([P, count], F32, tag="to_long")
+            to_short = work.tile([P, count], F32, tag="to_short")
             for push, switched_off in ((to_long, ALU.is_le), (to_short, ALU.is_gt)):
                 nc.gpsimd.tensor_scalar(
                     out=push[:], in0=abs_sum[:], scalar1=THRESHOLD * FEATURES, scalar2=-FAR,
                     op0=switched_off, op1=ALU.mult,
                 )
-            push1[pair], push2[pair] = to_long, to_short
+            push1[group], push2[group] = to_long, to_short
 
-        def quantise_x(pair):
-            codes = work.tile([P, PAIR, X_PASSES, P], U32, tag="x_codes", align_bytes=64)
-            scales = work.tile([P, PAIR, X_PASSES, P], U8, tag="x_scales", align_bytes=64)
+        def quantise_x(group):
+            count = GROUPS[group][1]
+            codes = work.tile([P, count, X_PASSES, P], U32, tag="x_codes", align_bytes=64)
+            scales = work.tile([P, count, X_PASSES, P], U8, tag="x_scales", align_bytes=64)
             nc.vector.quantize_mx(
                 out=codes[:].rearrange("p s g r -> p (s g r)").bitcast(FP8X4),
                 scales=scales[:].rearrange("p s g r -> p (s g r)"),
-                in_=x_grouped[pair][:].rearrange("p s k -> p (s k)"),
+                in_=x_grouped[group][:].rearrange("p s k -> p (s k)"),
             )
-            x_codes[pair], x_scales[pair] = codes, scales
+            x_codes[group], x_scales[group] = codes, scales
 
-        def first_layer(pair):
+        def first_layer(group):
+            count = GROUPS[group][1]
+
             def passes(acc, s, words_sb, scales_sb):
                 for g in range(X_PASSES):
                     nc.tensor.matmul_mx(
                         out=acc,
-                        lhsT=x_codes[pair][:, s, g, :].bitcast(FP8X4),
-                        lhsT_scale=x_scales[pair][:, s, g, :],
+                        lhsT=x_codes[group][:, s, g, :].bitcast(FP8X4),
+                        lhsT_scale=x_scales[group][:, s, g, :],
                         rhs=words_sb[:, g, :].bitcast(FP8X4),
                         rhs_scale=scales_sb[:, g, :],
                         start=(g == 0),
@@ -180,78 +185,81 @@ def tile_dynamiclayer_kernel(
                     )
 
             long_acc = []
-            for s in range(PAIR):
+            for s in range(count):
                 acc1 = psum.tile([P, HIDDEN], F32, tag="bank")
                 passes(acc1[:], s, w1_words, w1_scales)
                 long_acc.append(acc1)
-            acc2 = psum.tile([P, PAIR, HIDDEN2], F32, tag="bank")
-            for s in range(PAIR):
+            acc2 = psum.tile([P, count, HIDDEN2], F32, tag="bank")
+            for s in range(count):
                 passes(acc2[:, s, :], s, w2_words, w2_scales)
-            sorted_h = work.tile([P, PAIR, PACK, P], BF16, tag="h_sorted")
-            short = work.tile([P, PAIR, PACK, P2], BF16, tag="short")
-            for s in range(PAIR):
+            sorted_h = work.tile([P, count, PACK, P], BF16, tag="h_sorted")
+            short = work.tile([P, count, PACK, P2], BF16, tag="short")
+            for s in range(count):
                 nc.vector.scalar_tensor_tensor(
                     out=sorted_h[:, s], in0=long_acc[s][:].rearrange("r (p t) -> r t p", t=PACK),
-                    scalar=push1[pair][:, s : s + 1], in1=b1_sorted[:],
+                    scalar=push1[group][:, s : s + 1], in1=b1_sorted[:],
                     op0=ALU.add, op1=ALU.add,
                 )
-            for s in range(PAIR):
+            for s in range(count):
                 nc.vector.scalar_tensor_tensor(
                     out=short[:, s], in0=acc2[:, s, :].rearrange("r (p t) -> r t p", t=PACK),
-                    scalar=push2[pair][:, s : s + 1], in1=b2_sorted[:],
+                    scalar=push2[group][:, s : s + 1], in1=b2_sorted[:],
                     op0=ALU.add, op1=ALU.add,
                 )
             low = sorted_h[:].rearrange("r s t p -> r (s t) p")[:, :, 0:P2]
             nc.vector.tensor_tensor(out=low, in0=low, in1=short[:].rearrange("r s t p -> r (s t) p"), op=ALU.max)
-            h_sorted[pair] = sorted_h
+            h_sorted[group] = sorted_h
 
-        def transpose_h(pair):
-            ht = psum.tile([P, PAIR, PACK, P], BF16, tag="bank")
-            for s in range(PAIR):
+        def transpose_h(group):
+            count = GROUPS[group][1]
+            ht = psum.tile([P, count, PACK, P], BF16, tag="bank")
+            for s in range(count):
                 for t in range(PACK):
-                    nc.tensor.transpose(ht[:, s, t, :], h_sorted[pair][:, s, t, :], ident_bf16[:])
-            grouped = work.tile([P, PAIR, P, PACK], BF16, tag="h_grouped", align_bytes=64)
+                    nc.tensor.transpose(ht[:, s, t, :], h_sorted[group][:, s, t, :], ident_bf16[:])
+            grouped = work.tile([P, count, P, PACK], BF16, tag="h_grouped", align_bytes=64)
             nc.scalar.activation(out=grouped[:], in_=ht[:].rearrange("p s t r -> p s r t"), func=ACT.Relu)
-            h_grouped[pair] = grouped
+            h_grouped[group] = grouped
 
-        def quantise_h(pair):
-            codes = work.tile([P, PAIR, P], U32, tag="h_codes", align_bytes=64)
-            scales = work.tile([P, PAIR, P], U8, tag="h_scales", align_bytes=64)
+        def quantise_h(group):
+            count = GROUPS[group][1]
+            codes = work.tile([P, count, P], U32, tag="h_codes", align_bytes=64)
+            scales = work.tile([P, count, P], U8, tag="h_scales", align_bytes=64)
             nc.vector.quantize_mx(
                 out=codes[:].rearrange("p s r -> p (s r)").bitcast(FP8X4),
                 scales=scales[:].rearrange("p s r -> p (s r)"),
-                in_=h_grouped[pair][:].rearrange("p s r t -> p (s r t)"),
+                in_=h_grouped[group][:].rearrange("p s r t -> p (s r t)"),
             )
-            h_codes[pair], h_scales[pair] = codes, scales
+            h_codes[group], h_scales[group] = codes, scales
 
-        def last_layer(pair):
-            for s in range(PAIR):
+        def last_layer(group):
+            first_tile, count = GROUPS[group]
+            for s in range(count):
                 result = work.tile([P, OUT], F32, tag="result", bufs=4)
                 for first_col in range(0, OUT, BANK):
                     cols = slice(first_col, first_col + BANK)
                     acc = psum.tile([P, BANK], F32, tag="bank")
                     nc.tensor.matmul_mx(
                         out=acc[:],
-                        lhsT=h_codes[pair][:, s, :].bitcast(FP8X4),
-                        lhsT_scale=h_scales[pair][:, s, :],
+                        lhsT=h_codes[group][:, s, :].bitcast(FP8X4),
+                        lhsT_scale=h_scales[group][:, s, :],
                         rhs=wf_words[:, 0, cols].bitcast(FP8X4),
                         rhs_scale=wf_scales[:, 0, cols],
                         start=True,
                         stop=True,
                     )
-                    if s == 0 and first_col == BANK:
+                    if count == 2 and s == 0 and first_col == BANK:
                         nc.scalar.copy(out=result[:, cols], in_=acc[:])
                         nc.gpsimd.tensor_tensor(
                             out=result[:, cols], in0=result[:, cols], in1=bf_all[:, cols], op=ALU.add
                         )
                     else:
                         nc.vector.tensor_tensor(out=result[:, cols], in0=acc[:], in1=bf_all[:, cols], op=ALU.add)
-                    nc.sync.dma_start(out=out_rows[:, PAIR * pair + s, cols], in_=result[:, cols])
+                    nc.sync.dma_start(out=out_rows[:, first_tile + s, cols], in_=result[:, cols])
 
-        def in_range(pair):
-            return 0 <= pair < N_PAIRS
+        def in_range(group):
+            return 0 <= group < N_GROUPS
 
-        for j in range(N_PAIRS + 3):
+        for j in range(N_GROUPS + 3):
             if in_range(j):
                 transpose_x(j)
             if in_range(j - 2):

@@ -120,7 +120,7 @@ def tile_dynamiclayer_kernel(
                 nc.vector.tensor_copy(out=bf_all[:, first_col : first_col + BANK], in_=bf_bank[:])
 
         x_grouped, x_codes, x_scales = {}, {}, {}
-        h_sorted, h_grouped, h_codes, h_scales = {}, {}, {}, {}
+        h_sorted, h_short, h_grouped, h_codes, h_scales = {}, {}, {}, {}, {}
         push1, push2 = {}, {}
 
         def transpose_x(group):
@@ -206,9 +206,13 @@ def tile_dynamiclayer_kernel(
                     scalar=push2[group][:, s : s + 1], in1=b2_sorted[:],
                     op0=ALU.add, op1=ALU.add,
                 )
-            low = sorted_h[:].rearrange("r s t p -> r (s t) p")[:, :, 0:P2]
-            nc.vector.tensor_tensor(out=low, in0=low, in1=short[:].rearrange("r s t p -> r (s t) p"), op=ALU.max)
-            h_sorted[group] = sorted_h
+            h_sorted[group], h_short[group] = sorted_h, short
+
+        def merge_branches(group):
+            low = h_sorted[group][:].rearrange("r s t p -> r (s t) p")[:, :, 0:P2]
+            nc.vector.tensor_tensor(
+                out=low, in0=low, in1=h_short[group][:].rearrange("r s t p -> r (s t) p"), op=ALU.max
+            )
 
         def transpose_h(group):
             count = GROUPS[group][1]
@@ -270,6 +274,8 @@ def tile_dynamiclayer_kernel(
                 first_layer(j - 1)
             if in_range(j):
                 quantise_x(j)
+            if in_range(j - 1):
+                merge_branches(j - 1)
             if j == 0:
                 spread_first_biases()
             if j == 1:

@@ -44,19 +44,22 @@ def tile_dynamiclayer_kernel(
         psum = ctx.enter_context(tc.psum_pool(name="psum", bufs=N_BANKS))
 
         x_sb = keep.tile([P, N_TILES, FEATURES], BF16)
+        w1_words_raw = keep.tile([P, X_PASSES, HIDDEN], I32)
+        w2_words_raw = keep.tile([P, X_PASSES, HIDDEN2], I32)
+        w1_scales_raw = keep.tile([P, X_PASSES, HIDDEN], U8)
+        w2_scales_raw = keep.tile([P, X_PASSES, HIDDEN2], U8)
         w1_words = keep.tile([P, X_PASSES, HIDDEN], I32, align_bytes=64)
         w2_words = keep.tile([P, X_PASSES, HIDDEN2], I32, align_bytes=64)
-        wf_words = keep.tile([P, 1, OUT], I32, align_bytes=64)
         w1_scales = keep.tile([P, X_PASSES, HIDDEN], U8, align_bytes=64)
         w2_scales = keep.tile([P, X_PASSES, HIDDEN2], U8, align_bytes=64)
+        wf_words = keep.tile([P, 1, OUT], I32, align_bytes=64)
         wf_scales = keep.tile([P, 1, OUT], U8, align_bytes=64)
         bias_rows = keep.tile([P, HIDDEN + HIDDEN2 + OUT], BF16)
         ones = keep.tile([P, P], BF16)
-        b1_sorted = keep.tile([P, PACK, P], F32)
-        b2_sorted = keep.tile([P, PACK, P2], F32)
+        b1_sorted = keep.tile([P, HIDDEN], F32)
+        b2_sorted = keep.tile([P, HIDDEN2], F32)
         bf_all = keep.tile([P, OUT], F32)
         ident_f32 = keep.tile([P, P], F32)
-        ident_bf16 = keep.tile([P, P], BF16)
 
         def load_x(first, count):
             nc.sync.dma_start(out=x_sb[:, first : first + count, :], in_=x_rows[:, first : first + count, :])
@@ -84,10 +87,10 @@ def tile_dynamiclayer_kernel(
 
         load_x(*x_loads[0])
         load_x(*x_loads[1])
-        load_scales(w1_scales, W1_scales)
-        load_words(w1_words, W1_words)
-        load_words(w2_words, W2_words)
-        load_scales(w2_scales, W2_scales)
+        load_scales(w1_scales_raw, W1_scales)
+        load_words(w1_words_raw, W1_words)
+        load_words(w2_words_raw, W2_words)
+        load_scales(w2_scales_raw, W2_scales)
         load_x(*x_loads[2])
         load_scales(wf_scales, Wf_scales)
         load_words(wf_words, Wf_words)
@@ -99,7 +102,20 @@ def tile_dynamiclayer_kernel(
         for bias in (b1, b2, bf):
             nc.gpsimd.dma_start(out=bias_rows[0:1, first : first + bias.shape[0]], in_=bias.unsqueeze(0))
             first += bias.shape[0]
-        make_identity(nc, ident_bf16[:])
+
+        def sort_words(sorted_sb, raw_sb):
+            for g in range(X_PASSES):
+                nc.vector.tensor_copy(
+                    out=sorted_sb[:, g, :].rearrange("q (u p e) -> q u p e", u=2, e=2),
+                    in_=raw_sb[:, g, :].rearrange("q (p u e) -> q u p e", u=2, e=2),
+                )
+
+        def sort_scales(sorted_sb, raw_sb):
+            for g in range(X_PASSES):
+                nc.vector.tensor_copy(
+                    out=sorted_sb[:, g, :].rearrange("q (u p e) -> q p u e", u=2, e=2),
+                    in_=raw_sb[:, g, :].rearrange("q (p u e) -> q p u e", u=2, e=2),
+                )
 
         def spread_bias(first_col, width):
             bank = psum.tile([P, width], F32, tag="bank")
@@ -110,9 +126,15 @@ def tile_dynamiclayer_kernel(
 
         def spread_first_biases():
             b1_bank = spread_bias(0, HIDDEN)
-            nc.vector.tensor_copy(out=b1_sorted[:], in_=b1_bank[:].rearrange("r (p t) -> r t p", t=PACK))
+            nc.vector.tensor_copy(
+                out=b1_sorted[:].rearrange("r (u p e) -> r u p e", u=2, e=2),
+                in_=b1_bank[:].rearrange("r (p u e) -> r u p e", u=2, e=2),
+            )
             b2_bank = spread_bias(HIDDEN, HIDDEN2)
-            nc.vector.tensor_copy(out=b2_sorted[:], in_=b2_bank[:].rearrange("r (p t) -> r t p", t=PACK))
+            nc.vector.tensor_copy(
+                out=b2_sorted[:].rearrange("r (u p e) -> r u p e", u=2, e=2),
+                in_=b2_bank[:].rearrange("r (p u e) -> r u p e", u=2, e=2),
+            )
 
         def spread_last_bias():
             for first_col in range(0, OUT, BANK):
@@ -192,36 +214,42 @@ def tile_dynamiclayer_kernel(
             acc2 = psum.tile([P, count, HIDDEN2], F32, tag="bank")
             for s in range(count):
                 passes(acc2[:, s, :], s, w2_words, w2_scales)
-            sorted_h = work.tile([P, count, PACK, P], BF16, tag="h_sorted")
-            short = work.tile([P, count, PACK, P2], BF16, tag="short")
+            sorted_h = work.tile([P, count, HIDDEN], BF16, tag="h_sorted")
+            short = work.tile([P, count, HIDDEN2], BF16, tag="short")
             for s in range(count):
                 nc.vector.scalar_tensor_tensor(
-                    out=sorted_h[:, s], in0=long_acc[s][:].rearrange("r (p t) -> r t p", t=PACK),
+                    out=sorted_h[:, s, :], in0=long_acc[s][:],
                     scalar=push1[group][:, s : s + 1], in1=b1_sorted[:],
                     op0=ALU.add, op1=ALU.add,
                 )
             for s in range(count):
                 nc.vector.scalar_tensor_tensor(
-                    out=short[:, s], in0=acc2[:, s, :].rearrange("r (p t) -> r t p", t=PACK),
+                    out=short[:, s, :], in0=acc2[:, s, :],
                     scalar=push2[group][:, s : s + 1], in1=b2_sorted[:],
                     op0=ALU.add, op1=ALU.add,
                 )
             h_sorted[group], h_short[group] = sorted_h, short
 
         def merge_branches(group):
-            low = h_sorted[group][:].rearrange("r s t p -> r (s t) p")[:, :, 0:P2]
+            low = h_sorted[group][:].rearrange("r s (u n) -> r (s u) n", u=2)[:, :, 0 : 2 * P2]
             nc.vector.tensor_tensor(
-                out=low, in0=low, in1=h_short[group][:].rearrange("r s t p -> r (s t) p"), op=ALU.max
+                out=low, in0=low, in1=h_short[group][:].rearrange("r s (u n) -> r (s u) n", u=2), op=ALU.max
             )
 
         def transpose_h(group):
             count = GROUPS[group][1]
-            ht = psum.tile([P, count, PACK, P], BF16, tag="bank")
+            ht = psum.tile([P, count, 2, P], F32, tag="bank")
             for s in range(count):
-                for t in range(PACK):
-                    nc.tensor.transpose(ht[:, s, t, :], h_sorted[group][:, s, t, :], ident_bf16[:])
+                words = h_sorted[group][:, s, :].bitcast(F32)
+                for u in range(2):
+                    nc.tensor.transpose(ht[:, s, u, :], words[:, P * u : P * (u + 1)], ident_f32[:])
             grouped = work.tile([P, count, P, PACK], BF16, tag="h_grouped", align_bytes=64)
-            nc.scalar.activation(out=grouped[:], in_=ht[:].rearrange("p s t r -> p s r t"), func=ACT.Relu)
+            for s in range(count):
+                nc.scalar.activation(
+                    out=grouped[:, s].rearrange("p r (u e) -> p r u e", e=2),
+                    in_=ht[:, s].bitcast(BF16).rearrange("p u (r e) -> p r u e", e=2),
+                    func=ACT.Relu,
+                )
             h_grouped[group] = grouped
 
         def quantise_h(group):
@@ -270,6 +298,8 @@ def tile_dynamiclayer_kernel(
                 transpose_h(j - 2)
             if in_range(j):
                 choose_branch(j)
+            if j == 0:
+                sort_scales(w1_scales, w1_scales_raw)
             if in_range(j - 1):
                 first_layer(j - 1)
             if in_range(j):
@@ -277,6 +307,9 @@ def tile_dynamiclayer_kernel(
             if in_range(j - 1):
                 merge_branches(j - 1)
             if j == 0:
+                sort_words(w1_words, w1_words_raw)
+                sort_words(w2_words, w2_words_raw)
+                sort_scales(w2_scales, w2_scales_raw)
                 spread_first_biases()
             if j == 1:
                 spread_last_bias()

@@ -141,7 +141,7 @@ def tile_dynamiclayer_kernel(
                 bf_bank = spread_bias(HIDDEN + HIDDEN2 + first_col, BANK)
                 nc.vector.tensor_copy(out=bf_all[:, first_col : first_col + BANK], in_=bf_bank[:])
 
-        x_grouped, x_codes, x_scales = {}, {}, {}
+        x_banks, x_grouped, x_codes, x_scales = {}, {}, {}, {}
         h_sorted, h_short, h_grouped, h_codes, h_scales = {}, {}, {}, {}, {}
         push1, push2 = {}, {}
 
@@ -156,12 +156,14 @@ def tile_dynamiclayer_kernel(
                     for u in range(2):
                         nc.tensor.transpose(xt[:, g, u, :], words[:, 256 * g + u : 256 * (g + 1) : 2], ident_f32[:])
                 banks.append(xt)
-            for s in range(count):
+            x_banks[group], x_grouped[group] = banks, grouped
+
+        def copy_x(group):
+            for s in range(GROUPS[group][1]):
                 nc.scalar.copy(
-                    out=grouped[:, s, :].bitcast(F32).rearrange("p (g r u) -> p g r u", g=X_PASSES, u=2),
-                    in_=banks[s][:].rearrange("p g u r -> p g r u"),
+                    out=x_grouped[group][:, s, :].bitcast(F32).rearrange("p (g r u) -> p g r u", g=X_PASSES, u=2),
+                    in_=x_banks[group][s][:].rearrange("p g u r -> p g r u"),
                 )
-            x_grouped[group] = grouped
 
         def choose_branch(group):
             first_tile, count = GROUPS[group]
@@ -294,14 +296,14 @@ def tile_dynamiclayer_kernel(
         for j in range(N_GROUPS + 3):
             if in_range(j):
                 transpose_x(j)
-            if in_range(j - 2):
-                transpose_h(j - 2)
-            if in_range(j):
                 choose_branch(j)
+                copy_x(j)
             if j == 0:
                 sort_scales(w1_scales, w1_scales_raw)
             if in_range(j - 1):
                 first_layer(j - 1)
+            if in_range(j - 2):
+                transpose_h(j - 2)
             if in_range(j):
                 quantise_x(j)
             if in_range(j - 1):

@@ -237,6 +237,8 @@ def tile_dynamiclayer_kernel(
             nc.vector.tensor_tensor(
                 out=low, in0=low, in1=h_short[group][:].rearrange("r s (u n) -> r (s u) n", u=2), op=ALU.max
             )
+            whole = h_sorted[group][:].rearrange("r s n -> r (s n)")
+            nc.gpsimd.tensor_scalar(out=whole, in0=whole, scalar1=FAR, scalar2=0.0, op0=ALU.min, op1=ALU.max)
 
         def transpose_h(group):
             count = GROUPS[group][1]
@@ -246,12 +248,10 @@ def tile_dynamiclayer_kernel(
                 for u in range(2):
                     nc.tensor.transpose(ht[:, s, u, :], words[:, P * u : P * (u + 1)], ident_f32[:])
             grouped = work.tile([P, count, P, PACK], BF16, tag="h_grouped", align_bytes=64)
-            for s in range(count):
-                nc.scalar.activation(
-                    out=grouped[:, s].rearrange("p r (u e) -> p r u e", e=2),
-                    in_=ht[:, s].bitcast(BF16).rearrange("p u (r e) -> p r u e", e=2),
-                    func=ACT.Relu,
-                )
+            nc.scalar.copy(
+                out=grouped[:].rearrange("p s r t -> p s (r t)").bitcast(F32).rearrange("p s (r u) -> p s r u", u=2),
+                in_=ht[:].rearrange("p s u r -> p s r u"),
+            )
             h_grouped[group] = grouped
 
         def quantise_h(group):

@@ -237,8 +237,9 @@ def tile_dynamiclayer_kernel(
             nc.vector.tensor_tensor(
                 out=low, in0=low, in1=h_short[group][:].rearrange("r s (u n) -> r (s u) n", u=2), op=ALU.max
             )
-            whole = h_sorted[group][:].rearrange("r s n -> r (s n)")
-            nc.gpsimd.tensor_scalar(out=whole, in0=whole, scalar1=FAR, scalar2=0.0, op0=ALU.min, op1=ALU.max)
+            if GROUPS[group][1] == 2:
+                whole = h_sorted[group][:].rearrange("r s n -> r (s n)")
+                nc.gpsimd.tensor_scalar(out=whole, in0=whole, scalar1=FAR, scalar2=0.0, op0=ALU.min, op1=ALU.max)
 
         def transpose_h(group):
             count = GROUPS[group][1]
@@ -248,10 +249,17 @@ def tile_dynamiclayer_kernel(
                 for u in range(2):
                     nc.tensor.transpose(ht[:, s, u, :], words[:, P * u : P * (u + 1)], ident_f32[:])
             grouped = work.tile([P, count, P, PACK], BF16, tag="h_grouped", align_bytes=64)
-            nc.scalar.copy(
-                out=grouped[:].rearrange("p s r t -> p s (r t)").bitcast(F32).rearrange("p s (r u) -> p s r u", u=2),
-                in_=ht[:].rearrange("p s u r -> p s r u"),
-            )
+            if count == 2:
+                nc.scalar.copy(
+                    out=grouped[:].rearrange("p s r t -> p s (r t)").bitcast(F32).rearrange("p s (r u) -> p s r u", u=2),
+                    in_=ht[:].rearrange("p s u r -> p s r u"),
+                )
+            else:
+                nc.scalar.activation(
+                    out=grouped[:, 0].rearrange("p r (u e) -> p r u e", e=2),
+                    in_=ht[:, 0].bitcast(BF16).rearrange("p u (r e) -> p r u e", e=2),
+                    func=ACT.Relu,
+                )
             h_grouped[group] = grouped
 
         def quantise_h(group):

@@ -44,20 +44,18 @@ def tile_dynamiclayer_kernel(
         psum = ctx.enter_context(tc.psum_pool(name="psum", bufs=N_BANKS))
 
         x_sb = keep.tile([P, N_TILES, FEATURES], BF16)
-        w1_words_raw = keep.tile([P, X_PASSES, HIDDEN], I32)
-        w2_words_raw = keep.tile([P, X_PASSES, HIDDEN2], I32)
-        w1_scales_raw = keep.tile([P, X_PASSES, HIDDEN], U8)
-        w2_scales_raw = keep.tile([P, X_PASSES, HIDDEN2], U8)
         w1_words = keep.tile([P, X_PASSES, HIDDEN], I32, align_bytes=64)
         w2_words = keep.tile([P, X_PASSES, HIDDEN2], I32, align_bytes=64)
         w1_scales = keep.tile([P, X_PASSES, HIDDEN], U8, align_bytes=64)
         w2_scales = keep.tile([P, X_PASSES, HIDDEN2], U8, align_bytes=64)
         wf_words = keep.tile([P, 1, OUT], I32, align_bytes=64)
         wf_scales = keep.tile([P, 1, OUT], U8, align_bytes=64)
-        bias_rows = keep.tile([P, HIDDEN + HIDDEN2 + OUT], BF16)
-        ones = keep.tile([P, P], BF16)
-        b1_sorted = keep.tile([P, HIDDEN], F32)
-        b2_sorted = keep.tile([P, HIDDEN2], F32)
+        b1_raw = keep.tile([P, HIDDEN // P], BF16)
+        b2_raw = keep.tile([P, HIDDEN2 // P], BF16)
+        bf_raw = keep.tile([P, OUT // P], BF16)
+        ident_bf16 = keep.tile([P, P], BF16)
+        b1_all = keep.tile([P, HIDDEN], F32)
+        b2_all = keep.tile([P, HIDDEN2], F32)
         bf_all = keep.tile([P, OUT], F32)
         ident_f32 = keep.tile([P, P], F32)
 
@@ -65,7 +63,6 @@ def tile_dynamiclayer_kernel(
             nc.sync.dma_start(out=x_sb[:, first : first + count, :], in_=x_rows[:, first : first + count, :])
 
         def load_scales(scales_sb, scales):
-            nc.vector.memset(scales_sb[:].bitcast(I32), 0)
             for quadrant in range(4):
                 nc.sync.dma_start(
                     out=scales_sb[32 * quadrant : 32 * quadrant + 4].bitcast(I32),
@@ -75,71 +72,51 @@ def tile_dynamiclayer_kernel(
         def load_words(words_sb, words):
             nc.sync.dma_start(out=words_sb[:], in_=words.rearrange("g p n t -> p g (n t)").bitcast(I32))
 
-        x_loads = []
-        first = 0
-        while first < N_TILES:
-            count = min(max(first, 1), 4)
-            x_loads.append((first, count))
-            first += count
+        def load_bias(engine, raw, bias):
+            engine.dma_start(out=raw[:], in_=bias.rearrange("(p w) -> p w", p=P))
 
-        nc.vector.memset(bias_rows[:].bitcast(I32), 0)
-        nc.vector.memset(ones[:], 1.0)
+        for scales_sb in (w1_scales, w2_scales, wf_scales):
+            nc.vector.memset(scales_sb[:].bitcast(I32), 0)
 
-        load_x(*x_loads[0])
-        load_x(*x_loads[1])
-        load_scales(w1_scales_raw, W1_scales)
-        load_words(w1_words_raw, W1_words)
-        load_words(w2_words_raw, W2_words)
-        load_scales(w2_scales_raw, W2_scales)
-        load_x(*x_loads[2])
-        load_scales(wf_scales, Wf_scales)
+        load_x(0, 1)
+        load_bias(nc.scalar, b1_raw, b1)
+        load_bias(nc.scalar, b2_raw, b2)
+        load_x(1, 1)
+        load_words(w1_words, W1_words)
+        load_x(2, 2)
+        load_scales(w1_scales, W1_scales)
+        load_words(w2_words, W2_words)
+        load_scales(w2_scales, W2_scales)
+        load_x(4, 2)
+        load_bias(nc.sync, bf_raw, bf)
+        load_x(6, 2)
         load_words(wf_words, Wf_words)
-        for first, count in x_loads[3:]:
-            load_x(first, count)
+        load_scales(wf_scales, Wf_scales)
+        load_x(8, 4)
+        load_x(12, 4)
 
         make_identity(nc, ident_f32[:])
-        first = 0
-        for bias in (b1, b2, bf):
-            nc.gpsimd.dma_start(out=bias_rows[0:1, first : first + bias.shape[0]], in_=bias.unsqueeze(0))
-            first += bias.shape[0]
+        make_identity(nc, ident_bf16[:])
 
-        def sort_words(sorted_sb, raw_sb):
-            for g in range(X_PASSES):
-                nc.vector.tensor_copy(
-                    out=sorted_sb[:, g, :].rearrange("q (u p e) -> q u p e", u=2, e=2),
-                    in_=raw_sb[:, g, :].rearrange("q (p u e) -> q u p e", u=2, e=2),
+        def spread_bias(spread, raw, part=slice(None)):
+            values = raw[:, part]
+            width = values.shape[1]
+            bank = psum.tile([P, width, P], F32, tag="bank")
+            for w in range(width):
+                nc.tensor.matmul(
+                    out=bank[:, w, :], lhsT=values[:, w : w + 1].to_broadcast([P, P]), rhs=ident_bf16[:],
+                    start=True, stop=True,
                 )
-
-        def sort_scales(sorted_sb, raw_sb):
-            for g in range(X_PASSES):
-                nc.vector.tensor_copy(
-                    out=sorted_sb[:, g, :].rearrange("q (u p e) -> q p u e", u=2, e=2),
-                    in_=raw_sb[:, g, :].rearrange("q (p u e) -> q p u e", u=2, e=2),
-                )
-
-        def spread_bias(first_col, width):
-            bank = psum.tile([P, width], F32, tag="bank")
-            nc.tensor.matmul(
-                out=bank[:], lhsT=ones[:], rhs=bias_rows[:, first_col : first_col + width], start=True, stop=True
-            )
-            return bank
+            nc.vector.tensor_copy(out=spread, in_=bank[:].rearrange("r w p -> r p w"))
 
         def spread_first_biases():
-            b1_bank = spread_bias(0, HIDDEN)
-            nc.vector.tensor_copy(
-                out=b1_sorted[:].rearrange("r (u p e) -> r u p e", u=2, e=2),
-                in_=b1_bank[:].rearrange("r (p u e) -> r u p e", u=2, e=2),
-            )
-            b2_bank = spread_bias(HIDDEN, HIDDEN2)
-            nc.vector.tensor_copy(
-                out=b2_sorted[:].rearrange("r (u p e) -> r u p e", u=2, e=2),
-                in_=b2_bank[:].rearrange("r (p u e) -> r u p e", u=2, e=2),
-            )
+            spread_bias(b1_all[:].rearrange("r (p w) -> r p w", p=P), b1_raw)
+            spread_bias(b2_all[:].rearrange("r (p w) -> r p w", p=P), b2_raw)
 
         def spread_last_bias():
-            for first_col in range(0, OUT, BANK):
-                bf_bank = spread_bias(HIDDEN + HIDDEN2 + first_col, BANK)
-                nc.vector.tensor_copy(out=bf_all[:, first_col : first_col + BANK], in_=bf_bank[:])
+            half = OUT // P // 2
+            for part in (slice(0, half), slice(half, 2 * half)):
+                spread_bias(bf_all[:].rearrange("r (p w) -> r p w", p=P)[:, :, part], bf_raw, part)
 
         x_banks, x_grouped, x_codes, x_scales = {}, {}, {}, {}
         h_sorted, h_short, h_grouped, h_codes, h_scales = {}, {}, {}, {}, {}
@@ -169,10 +146,16 @@ def tile_dynamiclayer_kernel(
             first_tile, count = GROUPS[group]
             abs_sum = work.tile([P, count], F32, tag="abs_sum")
             for s in range(count):
-                magnitude = work.tile([P, FEATURES], BF16, tag="magnitude")
-                nc.scalar.activation(
-                    out=magnitude[:], in_=x_sb[:, first_tile + s, :], func=ACT.Abs, accum_out=abs_sum[:, s : s + 1]
-                )
+                if group == 0:
+                    nc.vector.tensor_reduce(
+                        out=abs_sum[:, s : s + 1], in_=x_sb[:, first_tile + s, :], axis=mybir.AxisListType.X,
+                        op=ALU.add, apply_absolute_value=True,
+                    )
+                else:
+                    magnitude = work.tile([P, FEATURES], BF16, tag="magnitude")
+                    nc.scalar.activation(
+                        out=magnitude[:], in_=x_sb[:, first_tile + s, :], func=ACT.Abs, accum_out=abs_sum[:, s : s + 1]
+                    )
             to_long = work.tile([P, count], F32, tag="to_long")
             to_short = work.tile([P, count], F32, tag="to_short")
             for push, switched_off in ((to_long, ALU.is_le), (to_short, ALU.is_gt)):
@@ -216,38 +199,43 @@ def tile_dynamiclayer_kernel(
             acc2 = psum.tile([P, count, HIDDEN2], F32, tag="bank")
             for s in range(count):
                 passes(acc2[:, s, :], s, w2_words, w2_scales)
-            sorted_h = work.tile([P, count, HIDDEN], BF16, tag="h_sorted")
-            short = work.tile([P, count, HIDDEN2], BF16, tag="short")
+            sorted_h = work.tile([P, count, 2, HIDDEN // 2], BF16, tag="h_sorted")
+            short = work.tile([P, count, 2, HIDDEN2 // 2], BF16, tag="short")
+
+            def of_u(row_of_units, u):
+                return row_of_units.rearrange("r (p u e) -> r u p e", u=2, e=2)[:, u]
+
             for s in range(count):
-                nc.vector.scalar_tensor_tensor(
-                    out=sorted_h[:, s, :], in0=long_acc[s][:],
-                    scalar=push1[group][:, s : s + 1], in1=b1_sorted[:],
-                    op0=ALU.add, op1=ALU.add,
-                )
+                for u in range(2):
+                    nc.vector.scalar_tensor_tensor(
+                        out=sorted_h[:, s, u, :].rearrange("r (p e) -> r p e", e=2), in0=of_u(long_acc[s][:], u),
+                        scalar=push1[group][:, s : s + 1], in1=of_u(b1_all[:], u),
+                        op0=ALU.add, op1=ALU.add,
+                    )
             for s in range(count):
-                nc.vector.scalar_tensor_tensor(
-                    out=short[:, s, :], in0=acc2[:, s, :],
-                    scalar=push2[group][:, s : s + 1], in1=b2_sorted[:],
-                    op0=ALU.add, op1=ALU.add,
-                )
+                for u in range(2):
+                    nc.vector.scalar_tensor_tensor(
+                        out=short[:, s, u, :].rearrange("r (p e) -> r p e", e=2), in0=of_u(acc2[:, s, :], u),
+                        scalar=push2[group][:, s : s + 1], in1=of_u(b2_all[:], u),
+                        op0=ALU.add, op1=ALU.add,
+                    )
             h_sorted[group], h_short[group] = sorted_h, short
 
         def merge_branches(group):
-            low = h_sorted[group][:].rearrange("r s (u n) -> r (s u) n", u=2)[:, :, 0 : 2 * P2]
+            low = h_sorted[group][:, :, :, 0 : 2 * P2].rearrange("r s u n -> r (s u) n")
             nc.vector.tensor_tensor(
-                out=low, in0=low, in1=h_short[group][:].rearrange("r s (u n) -> r (s u) n", u=2), op=ALU.max
+                out=low, in0=low, in1=h_short[group][:].rearrange("r s u n -> r (s u) n"), op=ALU.max
             )
             if GROUPS[group][1] == 2:
-                whole = h_sorted[group][:].rearrange("r s n -> r (s n)")
+                whole = h_sorted[group][:].rearrange("r s u n -> r (s u n)")
                 nc.gpsimd.tensor_scalar(out=whole, in0=whole, scalar1=FAR, scalar2=0.0, op0=ALU.min, op1=ALU.max)
 
         def transpose_h(group):
             count = GROUPS[group][1]
             ht = psum.tile([P, count, 2, P], F32, tag="bank")
             for s in range(count):
-                words = h_sorted[group][:, s, :].bitcast(F32)
                 for u in range(2):
-                    nc.tensor.transpose(ht[:, s, u, :], words[:, P * u : P * (u + 1)], ident_f32[:])
+                    nc.tensor.transpose(ht[:, s, u, :], h_sorted[group][:, s, u, :].bitcast(F32), ident_f32[:])
             grouped = work.tile([P, count, P, PACK], BF16, tag="h_grouped", align_bytes=64)
             if count == 2:
                 nc.scalar.copy(
@@ -304,10 +292,12 @@ def tile_dynamiclayer_kernel(
         for j in range(N_GROUPS + 3):
             if in_range(j):
                 transpose_x(j)
-                choose_branch(j)
-                copy_x(j)
-            if j == 0:
-                sort_scales(w1_scales, w1_scales_raw)
+                if j < 2:
+                    copy_x(j)
+                    choose_branch(j)
+                else:
+                    choose_branch(j)
+                    copy_x(j)
             if in_range(j - 1):
                 first_layer(j - 1)
             if in_range(j - 2):
@@ -317,9 +307,6 @@ def tile_dynamiclayer_kernel(
             if in_range(j - 1):
                 merge_branches(j - 1)
             if j == 0:
-                sort_words(w1_words, w1_words_raw)
-                sort_words(w2_words, w2_words_raw)
-                sort_scales(w2_scales, w2_scales_raw)
                 spread_first_biases()
             if j == 1:
                 spread_last_bias()

@@ -23,8 +23,10 @@ THRESHOLD = 1.0
 N_TILES = ROWS // P
 GROUPS = [(first, 2) for first in range(0, N_TILES - 2, 2)] + [(N_TILES - 2, 1), (N_TILES - 1, 1)]
 N_GROUPS = len(GROUPS)
+LAST_PAIR = N_GROUPS - 3
 X_PASSES = FEATURES // K_PASS
 P2 = HIDDEN2 // PACK
+RAW_GROUPS = 1
 FAR = 1.0e38
 
 FLOPS = 2 * ROWS * FEATURES * (HIDDEN + HIDDEN2) + 2 * ROWS * HIDDEN * OUT
@@ -44,6 +46,10 @@ def tile_dynamiclayer_kernel(
         psum = ctx.enter_context(tc.psum_pool(name="psum", bufs=N_BANKS))
 
         x_sb = keep.tile([P, N_TILES, FEATURES], BF16)
+        w1_words_raw = keep.tile([P, X_PASSES, HIDDEN], I32, align_bytes=64)
+        w2_words_raw = keep.tile([P, X_PASSES, HIDDEN2], I32, align_bytes=64)
+        w1_scales_raw = keep.tile([P, X_PASSES, HIDDEN], U8, align_bytes=64)
+        w2_scales_raw = keep.tile([P, X_PASSES, HIDDEN2], U8, align_bytes=64)
         w1_words = keep.tile([P, X_PASSES, HIDDEN], I32, align_bytes=64)
         w2_words = keep.tile([P, X_PASSES, HIDDEN2], I32, align_bytes=64)
         w1_scales = keep.tile([P, X_PASSES, HIDDEN], U8, align_bytes=64)
@@ -54,8 +60,8 @@ def tile_dynamiclayer_kernel(
         b2_raw = keep.tile([P, HIDDEN2 // P], BF16)
         bf_raw = keep.tile([P, OUT // P], BF16)
         ident_bf16 = keep.tile([P, P], BF16)
-        b1_all = keep.tile([P, HIDDEN], F32)
-        b2_all = keep.tile([P, HIDDEN2], F32)
+        b1_sorted = keep.tile([P, HIDDEN], F32)
+        b2_sorted = keep.tile([P, HIDDEN2], F32)
         bf_all = keep.tile([P, OUT], F32)
         ident_f32 = keep.tile([P, P], F32)
 
@@ -75,18 +81,18 @@ def tile_dynamiclayer_kernel(
         def load_bias(engine, raw, bias):
             engine.dma_start(out=raw[:], in_=bias.rearrange("(p w) -> p w", p=P))
 
-        for scales_sb in (w1_scales, w2_scales, wf_scales):
+        for scales_sb in (w1_scales_raw, w2_scales_raw, wf_scales):
             nc.vector.memset(scales_sb[:].bitcast(I32), 0)
 
         load_x(0, 1)
         load_bias(nc.scalar, b1_raw, b1)
         load_bias(nc.scalar, b2_raw, b2)
         load_x(1, 1)
-        load_words(w1_words, W1_words)
+        load_words(w1_words_raw, W1_words)
         load_x(2, 2)
-        load_scales(w1_scales, W1_scales)
-        load_words(w2_words, W2_words)
-        load_scales(w2_scales, W2_scales)
+        load_scales(w1_scales_raw, W1_scales)
+        load_words(w2_words_raw, W2_words)
+        load_scales(w2_scales_raw, W2_scales)
         load_x(4, 2)
         load_bias(nc.sync, bf_raw, bf)
         load_x(6, 2)
@@ -98,7 +104,21 @@ def tile_dynamiclayer_kernel(
         make_identity(nc, ident_f32[:])
         make_identity(nc, ident_bf16[:])
 
-        def spread_bias(spread, raw, part=slice(None)):
+        def sort_words(sorted_sb, raw_sb):
+            for g in range(X_PASSES):
+                nc.vector.tensor_copy(
+                    out=sorted_sb[:, g, :].rearrange("q (u p e) -> q u p e", u=2, e=2),
+                    in_=raw_sb[:, g, :].rearrange("q (p u e) -> q u p e", u=2, e=2),
+                )
+
+        def sort_scales(sorted_sb, raw_sb):
+            for g in range(X_PASSES):
+                nc.vector.tensor_copy(
+                    out=sorted_sb[:, g, :].rearrange("q (u p e) -> q p u e", u=2, e=2),
+                    in_=raw_sb[:, g, :].rearrange("q (p u e) -> q p u e", u=2, e=2),
+                )
+
+        def spread_bias(raw, part=slice(None)):
             values = raw[:, part]
             width = values.shape[1]
             bank = psum.tile([P, width, P], F32, tag="bank")
@@ -107,16 +127,27 @@ def tile_dynamiclayer_kernel(
                     out=bank[:, w, :], lhsT=values[:, w : w + 1].to_broadcast([P, P]), rhs=ident_bf16[:],
                     start=True, stop=True,
                 )
-            nc.vector.tensor_copy(out=spread, in_=bank[:].rearrange("r w p -> r p w"))
+            return bank
 
         def spread_first_biases():
-            spread_bias(b1_all[:].rearrange("r (p w) -> r p w", p=P), b1_raw)
-            spread_bias(b2_all[:].rearrange("r (p w) -> r p w", p=P), b2_raw)
+            b1_bank = spread_bias(b1_raw)
+            nc.vector.tensor_copy(
+                out=b1_sorted[:].rearrange("r (u p e) -> r u p e", u=2, e=2),
+                in_=b1_bank[:].rearrange("r (u e) p -> r u p e", u=2),
+            )
+            b2_bank = spread_bias(b2_raw)
+            nc.vector.tensor_copy(
+                out=b2_sorted[:].rearrange("r (u q e) -> r u q e", u=2, e=2),
+                in_=b2_bank[:].rearrange("r e (q u) -> r u q e", u=2),
+            )
 
         def spread_last_bias():
             half = OUT // P // 2
             for part in (slice(0, half), slice(half, 2 * half)):
-                spread_bias(bf_all[:].rearrange("r (p w) -> r p w", p=P)[:, :, part], bf_raw, part)
+                bf_bank = spread_bias(bf_raw, part)
+                nc.vector.tensor_copy(
+                    out=bf_all[:].rearrange("r (p w) -> r p w", p=P)[:, :, part], in_=bf_bank[:].rearrange("r w p -> r p w")
+                )
 
         x_banks, x_grouped, x_codes, x_scales = {}, {}, {}, {}
         h_sorted, h_short, h_grouped, h_codes, h_scales = {}, {}, {}, {}, {}
@@ -191,51 +222,58 @@ def tile_dynamiclayer_kernel(
                         stop=(g == X_PASSES - 1),
                     )
 
+            raw = group < RAW_GROUPS
+            long_weights = (w1_words_raw, w1_scales_raw) if raw else (w1_words, w1_scales)
+            short_weights = (w2_words_raw, w2_scales_raw) if raw else (w2_words, w2_scales)
             long_acc = []
             for s in range(count):
                 acc1 = psum.tile([P, HIDDEN], F32, tag="bank")
-                passes(acc1[:], s, w1_words, w1_scales)
-                long_acc.append(acc1)
+                passes(acc1[:], s, *long_weights)
+                long_acc.append(acc1[:])
             acc2 = psum.tile([P, count, HIDDEN2], F32, tag="bank")
             for s in range(count):
-                passes(acc2[:, s, :], s, w2_words, w2_scales)
-            sorted_h = work.tile([P, count, 2, HIDDEN // 2], BF16, tag="h_sorted")
-            short = work.tile([P, count, 2, HIDDEN2 // 2], BF16, tag="short")
+                passes(acc2[:, s, :], s, *short_weights)
+            sorted_h = work.tile([P, count, HIDDEN], BF16, tag="h_sorted")
+            short = work.tile([P, count, HIDDEN2], BF16, tag="short")
 
-            def of_u(row_of_units, u):
-                return row_of_units.rearrange("r (p u e) -> r u p e", u=2, e=2)[:, u]
+            def empty(out_row, acc, push, bias):
+                def add(out_part, acc_part, bias_part):
+                    nc.vector.scalar_tensor_tensor(
+                        out=out_part, in0=acc_part, scalar=push, in1=bias_part, op0=ALU.add, op1=ALU.add
+                    )
+
+                if not raw:
+                    add(out_row, acc, bias)
+                    return
+                for u in range(2):
+                    add(
+                        out_row.rearrange("r (u p e) -> r u p e", u=2, e=2)[:, u],
+                        acc.rearrange("r (p u e) -> r u p e", u=2, e=2)[:, u],
+                        bias.rearrange("r (u p e) -> r u p e", u=2, e=2)[:, u],
+                    )
 
             for s in range(count):
-                for u in range(2):
-                    nc.vector.scalar_tensor_tensor(
-                        out=sorted_h[:, s, u, :].rearrange("r (p e) -> r p e", e=2), in0=of_u(long_acc[s][:], u),
-                        scalar=push1[group][:, s : s + 1], in1=of_u(b1_all[:], u),
-                        op0=ALU.add, op1=ALU.add,
-                    )
+                empty(sorted_h[:, s, :], long_acc[s], push1[group][:, s : s + 1], b1_sorted[:])
             for s in range(count):
-                for u in range(2):
-                    nc.vector.scalar_tensor_tensor(
-                        out=short[:, s, u, :].rearrange("r (p e) -> r p e", e=2), in0=of_u(acc2[:, s, :], u),
-                        scalar=push2[group][:, s : s + 1], in1=of_u(b2_all[:], u),
-                        op0=ALU.add, op1=ALU.add,
-                    )
+                empty(short[:, s, :], acc2[:, s, :], push2[group][:, s : s + 1], b2_sorted[:])
             h_sorted[group], h_short[group] = sorted_h, short
 
         def merge_branches(group):
-            low = h_sorted[group][:, :, :, 0 : 2 * P2].rearrange("r s u n -> r (s u) n")
+            low = h_sorted[group][:].rearrange("r s (u n) -> r (s u) n", u=2)[:, :, 0 : 2 * P2]
             nc.vector.tensor_tensor(
-                out=low, in0=low, in1=h_short[group][:].rearrange("r s u n -> r (s u) n"), op=ALU.max
+                out=low, in0=low, in1=h_short[group][:].rearrange("r s (u n) -> r (s u) n", u=2), op=ALU.max
             )
             if GROUPS[group][1] == 2:
-                whole = h_sorted[group][:].rearrange("r s u n -> r (s u n)")
+                whole = h_sorted[group][:].rearrange("r s n -> r (s n)")
                 nc.gpsimd.tensor_scalar(out=whole, in0=whole, scalar1=FAR, scalar2=0.0, op0=ALU.min, op1=ALU.max)
 
         def transpose_h(group):
             count = GROUPS[group][1]
             ht = psum.tile([P, count, 2, P], F32, tag="bank")
             for s in range(count):
+                words = h_sorted[group][:, s, :].bitcast(F32)
                 for u in range(2):
-                    nc.tensor.transpose(ht[:, s, u, :], h_sorted[group][:, s, u, :].bitcast(F32), ident_f32[:])
+                    nc.tensor.transpose(ht[:, s, u, :], words[:, P * u : P * (u + 1)], ident_f32[:])
             grouped = work.tile([P, count, P, PACK], BF16, tag="h_grouped", align_bytes=64)
             if count == 2:
                 nc.scalar.copy(
@@ -277,7 +315,7 @@ def tile_dynamiclayer_kernel(
                         start=True,
                         stop=True,
                     )
-                    if count == 2 and s == 0 and first_col == BANK:
+                    if s == 0 and first_col == BANK and group < LAST_PAIR:
                         nc.scalar.copy(out=result[:, cols], in_=acc[:])
                         nc.gpsimd.tensor_tensor(
                             out=result[:, cols], in0=result[:, cols], in1=bf_all[:, cols], op=ALU.add
@@ -308,6 +346,11 @@ def tile_dynamiclayer_kernel(
                 merge_branches(j - 1)
             if j == 0:
                 spread_first_biases()
+            if j == RAW_GROUPS - 1:
+                sort_words(w1_words, w1_words_raw)
+                sort_scales(w1_scales, w1_scales_raw)
+                sort_words(w2_words, w2_words_raw)
+                sort_scales(w2_scales, w2_scales_raw)
             if j == 1:
                 spread_last_bias()
             if in_range(j - 2):

@@ -26,7 +26,6 @@ N_GROUPS = len(GROUPS)
 LAST_PAIR = N_GROUPS - 3
 X_PASSES = FEATURES // K_PASS
 P2 = HIDDEN2 // PACK
-RAW_GROUPS = 1
 FAR = 1.0e38
 
 FLOPS = 2 * ROWS * FEATURES * (HIDDEN + HIDDEN2) + 2 * ROWS * HIDDEN * OUT
@@ -46,10 +45,10 @@ def tile_dynamiclayer_kernel(
         psum = ctx.enter_context(tc.psum_pool(name="psum", bufs=N_BANKS))
 
         x_sb = keep.tile([P, N_TILES, FEATURES], BF16)
-        w1_words_raw = keep.tile([P, X_PASSES, HIDDEN], I32, align_bytes=64)
-        w2_words_raw = keep.tile([P, X_PASSES, HIDDEN2], I32, align_bytes=64)
-        w1_scales_raw = keep.tile([P, X_PASSES, HIDDEN], U8, align_bytes=64)
-        w2_scales_raw = keep.tile([P, X_PASSES, HIDDEN2], U8, align_bytes=64)
+        w1_words_raw = keep.tile([P, X_PASSES, HIDDEN], I32)
+        w2_words_raw = keep.tile([P, X_PASSES, HIDDEN2], I32)
+        w1_scales_raw = keep.tile([P, X_PASSES, HIDDEN], U8)
+        w2_scales_raw = keep.tile([P, X_PASSES, HIDDEN2], U8)
         w1_words = keep.tile([P, X_PASSES, HIDDEN], I32, align_bytes=64)
         w2_words = keep.tile([P, X_PASSES, HIDDEN2], I32, align_bytes=64)
         w1_scales = keep.tile([P, X_PASSES, HIDDEN], U8, align_bytes=64)
@@ -78,26 +77,26 @@ def tile_dynamiclayer_kernel(
         def load_words(words_sb, words):
             nc.sync.dma_start(out=words_sb[:], in_=words.rearrange("g p n t -> p g (n t)").bitcast(I32))
 
-        def load_bias(engine, raw, bias):
-            engine.dma_start(out=raw[:], in_=bias.rearrange("(p w) -> p w", p=P))
+        def load_bias(raw, bias):
+            nc.sync.dma_start(out=raw[:], in_=bias.rearrange("(p w) -> p w", p=P))
 
         for scales_sb in (w1_scales_raw, w2_scales_raw, wf_scales):
             nc.vector.memset(scales_sb[:].bitcast(I32), 0)
 
         load_x(0, 1)
-        load_bias(nc.scalar, b1_raw, b1)
-        load_bias(nc.scalar, b2_raw, b2)
+        load_scales(w1_scales_raw, W1_scales)
         load_x(1, 1)
         load_words(w1_words_raw, W1_words)
         load_x(2, 2)
-        load_scales(w1_scales_raw, W1_scales)
+        load_bias(b1_raw, b1)
+        load_bias(b2_raw, b2)
         load_words(w2_words_raw, W2_words)
         load_scales(w2_scales_raw, W2_scales)
         load_x(4, 2)
-        load_bias(nc.sync, bf_raw, bf)
-        load_x(6, 2)
-        load_words(wf_words, Wf_words)
+        load_bias(bf_raw, bf)
         load_scales(wf_scales, Wf_scales)
+        load_words(wf_words, Wf_words)
+        load_x(6, 2)
         load_x(8, 4)
         load_x(12, 4)
 
@@ -141,13 +140,13 @@ def tile_dynamiclayer_kernel(
                 in_=b2_bank[:].rearrange("r e (q u) -> r u q e", u=2),
             )
 
-        def spread_last_bias():
-            half = OUT // P // 2
-            for part in (slice(0, half), slice(half, 2 * half)):
-                bf_bank = spread_bias(bf_raw, part)
-                nc.vector.tensor_copy(
-                    out=bf_all[:].rearrange("r (p w) -> r p w", p=P)[:, :, part], in_=bf_bank[:].rearrange("r w p -> r p w")
-                )
+        def spread_last_bias(half):
+            width = OUT // P // 2
+            part = slice(half * width, (half + 1) * width)
+            bf_bank = spread_bias(bf_raw, part)
+            nc.vector.tensor_copy(
+                out=bf_all[:].rearrange("r (p w) -> r p w", p=P)[:, :, part], in_=bf_bank[:].rearrange("r w p -> r p w")
+            )
 
         x_banks, x_grouped, x_codes, x_scales = {}, {}, {}, {}
         h_sorted, h_short, h_grouped, h_codes, h_scales = {}, {}, {}, {}, {}
@@ -177,16 +176,10 @@ def tile_dynamiclayer_kernel(
             first_tile, count = GROUPS[group]
             abs_sum = work.tile([P, count], F32, tag="abs_sum")
             for s in range(count):
-                if group == 0:
-                    nc.vector.tensor_reduce(
-                        out=abs_sum[:, s : s + 1], in_=x_sb[:, first_tile + s, :], axis=mybir.AxisListType.X,
-                        op=ALU.add, apply_absolute_value=True,
-                    )
-                else:
-                    magnitude = work.tile([P, FEATURES], BF16, tag="magnitude")
-                    nc.scalar.activation(
-                        out=magnitude[:], in_=x_sb[:, first_tile + s, :], func=ACT.Abs, accum_out=abs_sum[:, s : s + 1]
-                    )
+                magnitude = work.tile([P, FEATURES], BF16, tag="magnitude")
+                nc.scalar.activation(
+                    out=magnitude[:], in_=x_sb[:, first_tile + s, :], func=ACT.Abs, accum_out=abs_sum[:, s : s + 1]
+                )
             to_long = work.tile([P, count], F32, tag="to_long")
             to_short = work.tile([P, count], F32, tag="to_short")
             for push, switched_off in ((to_long, ALU.is_le), (to_short, ALU.is_gt)):
@@ -222,40 +215,29 @@ def tile_dynamiclayer_kernel(
                         stop=(g == X_PASSES - 1),
                     )
 
-            raw = group < RAW_GROUPS
-            long_weights = (w1_words_raw, w1_scales_raw) if raw else (w1_words, w1_scales)
-            short_weights = (w2_words_raw, w2_scales_raw) if raw else (w2_words, w2_scales)
             long_acc = []
             for s in range(count):
                 acc1 = psum.tile([P, HIDDEN], F32, tag="bank")
-                passes(acc1[:], s, *long_weights)
-                long_acc.append(acc1[:])
+                passes(acc1[:], s, w1_words, w1_scales)
+                long_acc.append(acc1)
             acc2 = psum.tile([P, count, HIDDEN2], F32, tag="bank")
             for s in range(count):
-                passes(acc2[:, s, :], s, *short_weights)
+                passes(acc2[:, s, :], s, w2_words, w2_scales)
             sorted_h = work.tile([P, count, HIDDEN], BF16, tag="h_sorted")
             short = work.tile([P, count, HIDDEN2], BF16, tag="short")
 
-            def empty(out_row, acc, push, bias):
-                def add(out_part, acc_part, bias_part):
-                    nc.vector.scalar_tensor_tensor(
-                        out=out_part, in0=acc_part, scalar=push, in1=bias_part, op0=ALU.add, op1=ALU.add
-                    )
-
-                if not raw:
-                    add(out_row, acc, bias)
-                    return
-                for u in range(2):
-                    add(
-                        out_row.rearrange("r (u p e) -> r u p e", u=2, e=2)[:, u],
-                        acc.rearrange("r (p u e) -> r u p e", u=2, e=2)[:, u],
-                        bias.rearrange("r (u p e) -> r u p e", u=2, e=2)[:, u],
-                    )
-
             for s in range(count):
-                empty(sorted_h[:, s, :], long_acc[s], push1[group][:, s : s + 1], b1_sorted[:])
+                nc.vector.scalar_tensor_tensor(
+                    out=sorted_h[:, s, :], in0=long_acc[s][:],
+                    scalar=push1[group][:, s : s + 1], in1=b1_sorted[:],
+                    op0=ALU.add, op1=ALU.add,
+                )
             for s in range(count):
-                empty(short[:, s, :], acc2[:, s, :], push2[group][:, s : s + 1], b2_sorted[:])
+                nc.vector.scalar_tensor_tensor(
+                    out=short[:, s, :], in0=acc2[:, s, :],
+                    scalar=push2[group][:, s : s + 1], in1=b2_sorted[:],
+                    op0=ALU.add, op1=ALU.add,
+                )
             h_sorted[group], h_short[group] = sorted_h, short
 
         def merge_branches(group):
@@ -315,7 +297,8 @@ def tile_dynamiclayer_kernel(
                         start=True,
                         stop=True,
                     )
-                    if s == 0 and first_col == BANK and group < LAST_PAIR:
+                    through_scalar = 0 if group >= LAST_PAIR else 2 if group == LAST_PAIR - 1 else 1
+                    if first_col == BANK and s < through_scalar:
                         nc.scalar.copy(out=result[:, cols], in_=acc[:])
                         nc.gpsimd.tensor_tensor(
                             out=result[:, cols], in0=result[:, cols], in1=bf_all[:, cols], op=ALU.add
@@ -327,6 +310,7 @@ def tile_dynamiclayer_kernel(
         def in_range(group):
             return 0 <= group < N_GROUPS
 
+        sort_scales(w1_scales, w1_scales_raw)
         for j in range(N_GROUPS + 3):
             if in_range(j):
                 transpose_x(j)
@@ -336,6 +320,8 @@ def tile_dynamiclayer_kernel(
                 else:
                     choose_branch(j)
                     copy_x(j)
+            if j == 1:
+                spread_first_biases()
             if in_range(j - 1):
                 first_layer(j - 1)
             if in_range(j - 2):
@@ -345,14 +331,11 @@ def tile_dynamiclayer_kernel(
             if in_range(j - 1):
                 merge_branches(j - 1)
             if j == 0:
-                spread_first_biases()
-            if j == RAW_GROUPS - 1:
                 sort_words(w1_words, w1_words_raw)
-                sort_scales(w1_scales, w1_scales_raw)
                 sort_words(w2_words, w2_words_raw)
                 sort_scales(w2_scales, w2_scales_raw)
-            if j == 1:
-                spread_last_bias()
+            if j in (1, 2):
+                spread_last_bias(j - 1)
             if in_range(j - 2):
                 quantise_h(j - 2)
             if in_range(j - 3):

@@ -55,10 +55,9 @@ def tile_dynamiclayer_kernel(
         w2_scales = keep.tile([P, X_PASSES, HIDDEN2], U8, align_bytes=64)
         wf_words = keep.tile([P, 1, OUT], I32, align_bytes=64)
         wf_scales = keep.tile([P, 1, OUT], U8, align_bytes=64)
-        b1_raw = keep.tile([P, HIDDEN // P], BF16)
-        b2_raw = keep.tile([P, HIDDEN2 // P], BF16)
-        bf_raw = keep.tile([P, OUT // P], BF16)
-        ident_bf16 = keep.tile([P, P], BF16)
+        first_biases = keep.tile([P, HIDDEN + HIDDEN2], BF16)
+        last_bias = keep.tile([P, OUT], BF16)
+        ones = keep.tile([P, P], BF16)
         b1_sorted = keep.tile([P, HIDDEN], F32)
         b2_sorted = keep.tile([P, HIDDEN2], F32)
         bf_all = keep.tile([P, OUT], F32)
@@ -77,23 +76,27 @@ def tile_dynamiclayer_kernel(
         def load_words(words_sb, words):
             nc.sync.dma_start(out=words_sb[:], in_=words.rearrange("g p n t -> p g (n t)").bitcast(I32))
 
-        def load_bias(raw, bias):
-            nc.sync.dma_start(out=raw[:], in_=bias.rearrange("(p w) -> p w", p=P))
+        def load_bias(row, bias):
+            nc.sync.dma_start(out=row, in_=bias.unsqueeze(0))
 
-        for scales_sb in (w1_scales_raw, w2_scales_raw, wf_scales):
-            nc.vector.memset(scales_sb[:].bitcast(I32), 0)
+        nc.vector.memset(w1_scales_raw[:].bitcast(I32), 0)
+        nc.vector.memset(first_biases[:].bitcast(I32), 0)
+        nc.vector.memset(w2_scales_raw[:].bitcast(I32), 0)
+        nc.vector.memset(ones[:], 1.0)
+        nc.vector.memset(last_bias[:].bitcast(I32), 0)
+        nc.vector.memset(wf_scales[:].bitcast(I32), 0)
 
         load_x(0, 1)
         load_scales(w1_scales_raw, W1_scales)
         load_x(1, 1)
         load_words(w1_words_raw, W1_words)
         load_x(2, 2)
-        load_bias(b1_raw, b1)
-        load_bias(b2_raw, b2)
+        load_bias(first_biases[0:1, 0:HIDDEN], b1)
+        load_bias(first_biases[0:1, HIDDEN:], b2)
         load_words(w2_words_raw, W2_words)
         load_scales(w2_scales_raw, W2_scales)
         load_x(4, 2)
-        load_bias(bf_raw, bf)
+        load_bias(last_bias[0:1, :], bf)
         load_scales(wf_scales, Wf_scales)
         load_words(wf_words, Wf_words)
         load_x(6, 2)
@@ -101,7 +104,6 @@ def tile_dynamiclayer_kernel(
         load_x(12, 4)
 
         make_identity(nc, ident_f32[:])
-        make_identity(nc, ident_bf16[:])
 
         def sort_words(sorted_sb, raw_sb):
             for g in range(X_PASSES):
@@ -117,40 +119,29 @@ def tile_dynamiclayer_kernel(
                     in_=raw_sb[:, g, :].rearrange("q (p u e) -> q p u e", u=2, e=2),
                 )
 
-        def spread_bias(raw, part=slice(None)):
-            values = raw[:, part]
-            width = values.shape[1]
-            bank = psum.tile([P, width, P], F32, tag="bank")
-            for w in range(width):
-                nc.tensor.matmul(
-                    out=bank[:, w, :], lhsT=values[:, w : w + 1].to_broadcast([P, P]), rhs=ident_bf16[:],
-                    start=True, stop=True,
-                )
+        def spread_bias(rows):
+            bank = psum.tile([P, rows.shape[1]], F32, tag="bank")
+            nc.tensor.matmul(out=bank[:], lhsT=ones[:], rhs=rows, start=True, stop=True)
             return bank
 
         def spread_first_biases():
-            b1_bank = spread_bias(b1_raw)
-            nc.vector.tensor_copy(
-                out=b1_sorted[:].rearrange("r (u p e) -> r u p e", u=2, e=2),
-                in_=b1_bank[:].rearrange("r (u e) p -> r u p e", u=2),
-            )
-            b2_bank = spread_bias(b2_raw)
-            nc.vector.tensor_copy(
-                out=b2_sorted[:].rearrange("r (u q e) -> r u q e", u=2, e=2),
-                in_=b2_bank[:].rearrange("r e (q u) -> r u q e", u=2),
-            )
+            for spread, rows in (
+                (b1_sorted, first_biases[:, 0:HIDDEN]), (b2_sorted, first_biases[:, HIDDEN : HIDDEN + HIDDEN2]),
+            ):
+                bank = spread_bias(rows)
+                nc.vector.tensor_copy(
+                    out=spread[:].rearrange("r (u p e) -> r u p e", u=2, e=2),
+                    in_=bank[:].rearrange("r (p u e) -> r u p e", u=2, e=2),
+                )
 
         def spread_last_bias(half):
-            width = OUT // P // 2
-            part = slice(half * width, (half + 1) * width)
-            bf_bank = spread_bias(bf_raw, part)
-            nc.vector.tensor_copy(
-                out=bf_all[:].rearrange("r (p w) -> r p w", p=P)[:, :, part], in_=bf_bank[:].rearrange("r w p -> r p w")
-            )
+            cols = slice(half * BANK, (half + 1) * BANK)
+            bank = spread_bias(last_bias[:, cols])
+            nc.vector.tensor_copy(out=bf_all[:, cols], in_=bank[:])
 
         x_banks, x_grouped, x_codes, x_scales = {}, {}, {}, {}
         h_sorted, h_short, h_grouped, h_codes, h_scales = {}, {}, {}, {}, {}
-        push1, push2 = {}, {}
+        abs_sums, push1, push2 = {}, {}, {}
 
         def transpose_x(group):
             first_tile, count = GROUPS[group]
@@ -172,19 +163,29 @@ def tile_dynamiclayer_kernel(
                     in_=x_banks[group][s][:].rearrange("p g u r -> p g r u"),
                 )
 
-        def choose_branch(group):
+        def sum_magnitudes(group):
             first_tile, count = GROUPS[group]
             abs_sum = work.tile([P, count], F32, tag="abs_sum")
             for s in range(count):
-                magnitude = work.tile([P, FEATURES], BF16, tag="magnitude")
-                nc.scalar.activation(
-                    out=magnitude[:], in_=x_sb[:, first_tile + s, :], func=ACT.Abs, accum_out=abs_sum[:, s : s + 1]
-                )
+                if first_tile + s == 1:
+                    nc.vector.tensor_reduce(
+                        out=abs_sum[:, s : s + 1], in_=x_sb[:, first_tile + s, :], axis=mybir.AxisListType.X,
+                        op=ALU.add, apply_absolute_value=True,
+                    )
+                else:
+                    magnitude = work.tile([P, FEATURES], BF16, tag="magnitude")
+                    nc.scalar.activation(
+                        out=magnitude[:], in_=x_sb[:, first_tile + s, :], func=ACT.Abs, accum_out=abs_sum[:, s : s + 1]
+                    )
+            abs_sums[group] = abs_sum
+
+        def make_pushes(group):
+            count = GROUPS[group][1]
             to_long = work.tile([P, count], F32, tag="to_long")
             to_short = work.tile([P, count], F32, tag="to_short")
             for push, switched_off in ((to_long, ALU.is_le), (to_short, ALU.is_gt)):
-                nc.gpsimd.tensor_scalar(
-                    out=push[:], in0=abs_sum[:], scalar1=THRESHOLD * FEATURES, scalar2=-FAR,
+                nc.vector.tensor_scalar(
+                    out=push[:], in0=abs_sums[group][:], scalar1=THRESHOLD * FEATURES, scalar2=-FAR,
                     op0=switched_off, op1=ALU.mult,
                 )
             push1[group], push2[group] = to_long, to_short
@@ -297,8 +298,7 @@ def tile_dynamiclayer_kernel(
                         start=True,
                         stop=True,
                     )
-                    through_scalar = 0 if group >= LAST_PAIR else 2 if group == LAST_PAIR - 1 else 1
-                    if first_col == BANK and s < through_scalar:
+                    if group < LAST_PAIR and s == 0 and first_col == BANK:
                         nc.scalar.copy(out=result[:, cols], in_=acc[:])
                         nc.gpsimd.tensor_tensor(
                             out=result[:, cols], in0=result[:, cols], in1=bf_all[:, cols], op=ALU.add
@@ -314,11 +314,11 @@ def tile_dynamiclayer_kernel(
         for j in range(N_GROUPS + 3):
             if in_range(j):
                 transpose_x(j)
-                if j < 2:
+                if j == 1:
                     copy_x(j)
-                    choose_branch(j)
+                    sum_magnitudes(j)
                 else:
-                    choose_branch(j)
+                    sum_magnitudes(j)
                     copy_x(j)
             if j == 1:
                 spread_first_biases()
@@ -328,6 +328,7 @@ def tile_dynamiclayer_kernel(
                 transpose_h(j - 2)
             if in_range(j):
                 quantise_x(j)
+                make_pushes(j)
             if in_range(j - 1):
                 merge_branches(j - 1)
             if j == 0:

@@ -57,7 +57,7 @@ def tile_dynamiclayer_kernel(
         wf_scales = keep.tile([P, 1, OUT], U8, align_bytes=64)
         first_biases = keep.tile([P, HIDDEN + HIDDEN2], BF16)
         last_bias = keep.tile([P, OUT], BF16)
-        ones = keep.tile([P, P], BF16)
+        ones = keep.tile([P, BANK], BF16)
         b1_sorted = keep.tile([P, HIDDEN], F32)
         b2_sorted = keep.tile([P, HIDDEN2], F32)
         bf_all = keep.tile([P, OUT], F32)
@@ -79,20 +79,20 @@ def tile_dynamiclayer_kernel(
         def load_bias(row, bias):
             nc.sync.dma_start(out=row, in_=bias.unsqueeze(0))
 
+        nc.vector.memset(ones[:], 1.0)
         nc.vector.memset(w1_scales_raw[:].bitcast(I32), 0)
         nc.vector.memset(first_biases[:].bitcast(I32), 0)
         nc.vector.memset(w2_scales_raw[:].bitcast(I32), 0)
-        nc.vector.memset(ones[:], 1.0)
         nc.vector.memset(last_bias[:].bitcast(I32), 0)
         nc.vector.memset(wf_scales[:].bitcast(I32), 0)
 
         load_x(0, 1)
-        load_scales(w1_scales_raw, W1_scales)
         load_x(1, 1)
+        load_scales(w1_scales_raw, W1_scales)
         load_words(w1_words_raw, W1_words)
-        load_x(2, 2)
         load_bias(first_biases[0:1, 0:HIDDEN], b1)
         load_bias(first_biases[0:1, HIDDEN:], b2)
+        load_x(2, 2)
         load_words(w2_words_raw, W2_words)
         load_scales(w2_scales_raw, W2_scales)
         load_x(4, 2)
@@ -121,8 +121,13 @@ def tile_dynamiclayer_kernel(
 
         def spread_bias(rows):
             bank = psum.tile([P, rows.shape[1]], F32, tag="bank")
-            nc.tensor.matmul(out=bank[:], lhsT=ones[:], rhs=rows, start=True, stop=True)
+            nc.tensor.matmul(out=bank[:], lhsT=ones[:, 0:P], rhs=rows, start=True, stop=True)
             return bank
+
+        def keep_busy(count):
+            bank = psum.tile([P, BANK], F32, tag="bank")
+            for turn in range(count):
+                nc.tensor.matmul(out=bank[:], lhsT=ones[:, 0:P], rhs=ones[:], start=True, stop=True)
 
         def spread_first_biases():
             for spread, rows in (
@@ -163,21 +168,23 @@ def tile_dynamiclayer_kernel(
                     in_=x_banks[group][s][:].rearrange("p g u r -> p g r u"),
                 )
 
-        def sum_magnitudes(group):
+        def sum_magnitudes(group, tiles):
             first_tile, count = GROUPS[group]
-            abs_sum = work.tile([P, count], F32, tag="abs_sum")
-            for s in range(count):
+            if group not in abs_sums:
+                abs_sum = work.tile([P, count], F32, tag="abs_sum")
+                abs_sums[group] = abs_sum
+            for s in tiles:
+                abs_sum = abs_sums[group][:, s : s + 1]
                 if first_tile + s == 1:
                     nc.vector.tensor_reduce(
-                        out=abs_sum[:, s : s + 1], in_=x_sb[:, first_tile + s, :], axis=mybir.AxisListType.X,
+                        out=abs_sum, in_=x_sb[:, first_tile + s, :], axis=mybir.AxisListType.X,
                         op=ALU.add, apply_absolute_value=True,
                     )
                 else:
                     magnitude = work.tile([P, FEATURES], BF16, tag="magnitude")
                     nc.scalar.activation(
-                        out=magnitude[:], in_=x_sb[:, first_tile + s, :], func=ACT.Abs, accum_out=abs_sum[:, s : s + 1]
+                        out=magnitude[:], in_=x_sb[:, first_tile + s, :], func=ACT.Abs, accum_out=abs_sum
                     )
-            abs_sums[group] = abs_sum
 
         def make_pushes(group):
             count = GROUPS[group][1]
@@ -311,17 +318,17 @@ def tile_dynamiclayer_kernel(
             return 0 <= group < N_GROUPS
 
         sort_scales(w1_scales, w1_scales_raw)
+        keep_busy(4)
         for j in range(N_GROUPS + 3):
             if in_range(j):
                 transpose_x(j)
-                if j == 1:
-                    copy_x(j)
-                    sum_magnitudes(j)
-                else:
-                    sum_magnitudes(j)
-                    copy_x(j)
-            if j == 1:
-                spread_first_biases()
+                if j == 0:
+                    keep_busy(3)
+                tiles = range(GROUPS[j][1])
+                early = 1 if j == 1 else len(tiles)
+                sum_magnitudes(j, tiles[:early])
+                copy_x(j)
+                sum_magnitudes(j, tiles[early:])
             if in_range(j - 1):
                 first_layer(j - 1)
             if in_range(j - 2):
@@ -333,6 +340,7 @@ def tile_dynamiclayer_kernel(
                 merge_branches(j - 1)
             if j == 0:
                 sort_words(w1_words, w1_words_raw)
+                spread_first_biases()
                 sort_words(w2_words, w2_words_raw)
                 sort_scales(w2_scales, w2_scales_raw)
             if j in (1, 2):

from contextlib import ExitStack

import concourse.mybir as mybir
from concourse.masks import make_identity

F32 = mybir.dt.float32
BF16 = mybir.dt.bfloat16
I32 = mybir.dt.int32
U32 = mybir.dt.uint32
U8 = mybir.dt.uint8
FP8X4 = mybir.dt.float8_e4m3fn_x4
ALU = mybir.AluOpType
ACT = mybir.ActivationFunctionType

P = 128
PACK = 4
K_PASS = P * PACK
BANK = 512
N_BANKS = 8

ROWS, FEATURES, HIDDEN, HIDDEN2, OUT = 2048, 1024, 512, 256, 1024
THRESHOLD = 1.0
N_TILES = ROWS // P
GROUPS = [(first, 2) for first in range(0, N_TILES - 2, 2)] + [(N_TILES - 2, 1), (N_TILES - 1, 1)]
N_GROUPS = len(GROUPS)
LAST_PAIR = N_GROUPS - 3
X_PASSES = FEATURES // K_PASS
P2 = HIDDEN2 // PACK
FAR = 1.0e38

FLOPS = 2 * ROWS * FEATURES * (HIDDEN + HIDDEN2) + 2 * ROWS * HIDDEN * OUT


def tile_dynamiclayer_kernel(
    tc, x, W1_words, W1_scales, b1, W2_words, W2_scales, b2, Wf_words, Wf_scales, bf, out
):
    nc = tc.nc
    x_rows = x.rearrange("(p i) k -> p i k", i=N_TILES)
    out_rows = out.rearrange("(p i) n -> p i n", i=N_TILES)

    with ExitStack() as ctx:
        ctx.enter_context(tc.manual_schedule())
        keep = ctx.enter_context(tc.tile_pool(name="keep", bufs=1))
        work = ctx.enter_context(tc.tile_pool(name="work", bufs=3))
        psum = ctx.enter_context(tc.psum_pool(name="psum", bufs=N_BANKS))

        x_sb = keep.tile([P, N_TILES, FEATURES], BF16)
        w1_words_raw = keep.tile([P, X_PASSES, HIDDEN], I32)
        w2_words_raw = keep.tile([P, X_PASSES, HIDDEN2], I32)
        w1_scales_raw = keep.tile([P, X_PASSES, HIDDEN], U8)
        w2_scales_raw = keep.tile([P, X_PASSES, HIDDEN2], U8)
        w1_words = keep.tile([P, X_PASSES, HIDDEN], I32, align_bytes=64)
        w2_words = keep.tile([P, X_PASSES, HIDDEN2], I32, align_bytes=64)
        w1_scales = keep.tile([P, X_PASSES, HIDDEN], U8, align_bytes=64)
        w2_scales = keep.tile([P, X_PASSES, HIDDEN2], U8, align_bytes=64)
        wf_words = keep.tile([P, 1, OUT], I32, align_bytes=64)
        wf_scales = keep.tile([P, 1, OUT], U8, align_bytes=64)
        first_biases = keep.tile([P, HIDDEN + HIDDEN2], BF16)
        last_bias = keep.tile([P, OUT], BF16)
        ones = keep.tile([P, BANK], BF16)
        b1_sorted = keep.tile([P, HIDDEN], F32)
        b2_sorted = keep.tile([P, HIDDEN2], F32)
        bf_all = keep.tile([P, OUT], F32)
        ident_f32 = keep.tile([P, P], F32)

        def load_x(first, count):
            nc.sync.dma_start(out=x_sb[:, first : first + count, :], in_=x_rows[:, first : first + count, :])

        def load_scales(scales_sb, scales):
            for quadrant in range(4):
                nc.sync.dma_start(
                    out=scales_sb[32 * quadrant : 32 * quadrant + 4].bitcast(I32),
                    in_=scales[:, 4 * quadrant : 4 * quadrant + 4, :].rearrange("g r n -> r g n").bitcast(I32),
                )

        def load_words(words_sb, words):
            nc.sync.dma_start(out=words_sb[:], in_=words.rearrange("g p n t -> p g (n t)").bitcast(I32))

        def load_bias(row, bias):
            nc.sync.dma_start(out=row, in_=bias.unsqueeze(0))

        nc.vector.memset(ones[:], 1.0)
        nc.vector.memset(w1_scales_raw[:].bitcast(I32), 0)
        nc.vector.memset(first_biases[:].bitcast(I32), 0)
        nc.vector.memset(w2_scales_raw[:].bitcast(I32), 0)
        nc.vector.memset(last_bias[:].bitcast(I32), 0)
        nc.vector.memset(wf_scales[:].bitcast(I32), 0)

        load_x(0, 1)
        load_x(1, 1)
        load_scales(w1_scales_raw, W1_scales)
        load_words(w1_words_raw, W1_words)
        load_bias(first_biases[0:1, 0:HIDDEN], b1)
        load_bias(first_biases[0:1, HIDDEN:], b2)
        load_x(2, 2)
        load_words(w2_words_raw, W2_words)
        load_scales(w2_scales_raw, W2_scales)
        load_x(4, 2)
        load_bias(last_bias[0:1, :], bf)
        load_scales(wf_scales, Wf_scales)
        load_words(wf_words, Wf_words)
        load_x(6, 2)
        load_x(8, 4)
        load_x(12, 4)

        make_identity(nc, ident_f32[:])

        def sort_words(sorted_sb, raw_sb):
            for g in range(X_PASSES):
                nc.vector.tensor_copy(
                    out=sorted_sb[:, g, :].rearrange("q (u p e) -> q u p e", u=2, e=2),
                    in_=raw_sb[:, g, :].rearrange("q (p u e) -> q u p e", u=2, e=2),
                )

        def sort_scales(sorted_sb, raw_sb):
            for g in range(X_PASSES):
                nc.vector.tensor_copy(
                    out=sorted_sb[:, g, :].rearrange("q (u p e) -> q p u e", u=2, e=2),
                    in_=raw_sb[:, g, :].rearrange("q (p u e) -> q p u e", u=2, e=2),
                )

        def spread_bias(rows):
            bank = psum.tile([P, rows.shape[1]], F32, tag="bank")
            nc.tensor.matmul(out=bank[:], lhsT=ones[:, 0:P], rhs=rows, start=True, stop=True)
            return bank

        def keep_busy(count):
            bank = psum.tile([P, BANK], F32, tag="bank")
            for turn in range(count):
                nc.tensor.matmul(out=bank[:], lhsT=ones[:, 0:P], rhs=ones[:], start=True, stop=True)

        def spread_first_biases():
            for spread, rows in (
                (b1_sorted, first_biases[:, 0:HIDDEN]), (b2_sorted, first_biases[:, HIDDEN : HIDDEN + HIDDEN2]),
            ):
                bank = spread_bias(rows)
                nc.vector.tensor_copy(
                    out=spread[:].rearrange("r (u p e) -> r u p e", u=2, e=2),
                    in_=bank[:].rearrange("r (p u e) -> r u p e", u=2, e=2),
                )

        def spread_last_bias(half):
            cols = slice(half * BANK, (half + 1) * BANK)
            bank = spread_bias(last_bias[:, cols])
            nc.vector.tensor_copy(out=bf_all[:, cols], in_=bank[:])

        x_banks, x_grouped, x_codes, x_scales = {}, {}, {}, {}
        h_sorted, h_short, h_grouped, h_codes, h_scales = {}, {}, {}, {}, {}
        abs_sums, push1, push2 = {}, {}, {}

        def transpose_x(group):
            first_tile, count = GROUPS[group]
            grouped = work.tile([P, count, FEATURES], BF16, tag="x_grouped", align_bytes=64)
            banks = []
            for s in range(count):
                words = x_sb[:, first_tile + s, :].bitcast(F32)
                xt = psum.tile([P, X_PASSES, 2, P], F32, tag="bank")
                for g in range(X_PASSES):
                    for u in range(2):
                        nc.tensor.transpose(xt[:, g, u, :], words[:, 256 * g + u : 256 * (g + 1) : 2], ident_f32[:])
                banks.append(xt)
            x_banks[group], x_grouped[group] = banks, grouped

        def copy_x(group):
            for s in range(GROUPS[group][1]):
                nc.scalar.copy(
                    out=x_grouped[group][:, s, :].bitcast(F32).rearrange("p (g r u) -> p g r u", g=X_PASSES, u=2),
                    in_=x_banks[group][s][:].rearrange("p g u r -> p g r u"),
                )

        def sum_magnitudes(group, tiles):
            first_tile, count = GROUPS[group]
            if group not in abs_sums:
                abs_sum = work.tile([P, count], F32, tag="abs_sum")
                abs_sums[group] = abs_sum
            for s in tiles:
                abs_sum = abs_sums[group][:, s : s + 1]
                if first_tile + s == 1:
                    nc.vector.tensor_reduce(
                        out=abs_sum, in_=x_sb[:, first_tile + s, :], axis=mybir.AxisListType.X,
                        op=ALU.add, apply_absolute_value=True,
                    )
                else:
                    magnitude = work.tile([P, FEATURES], BF16, tag="magnitude")
                    nc.scalar.activation(
                        out=magnitude[:], in_=x_sb[:, first_tile + s, :], func=ACT.Abs, accum_out=abs_sum
                    )

        def make_pushes(group):
            count = GROUPS[group][1]
            to_long = work.tile([P, count], F32, tag="to_long")
            to_short = work.tile([P, count], F32, tag="to_short")
            for push, switched_off in ((to_long, ALU.is_le), (to_short, ALU.is_gt)):
                nc.vector.tensor_scalar(
                    out=push[:], in0=abs_sums[group][:], scalar1=THRESHOLD * FEATURES, scalar2=-FAR,
                    op0=switched_off, op1=ALU.mult,
                )
            push1[group], push2[group] = to_long, to_short

        def quantise_x(group):
            count = GROUPS[group][1]
            codes = work.tile([P, count, X_PASSES, P], U32, tag="x_codes", align_bytes=64)
            scales = work.tile([P, count, X_PASSES, P], U8, tag="x_scales", align_bytes=64)
            nc.vector.quantize_mx(
                out=codes[:].rearrange("p s g r -> p (s g r)").bitcast(FP8X4),
                scales=scales[:].rearrange("p s g r -> p (s g r)"),
                in_=x_grouped[group][:].rearrange("p s k -> p (s k)"),
            )
            x_codes[group], x_scales[group] = codes, scales

        def first_layer(group):
            count = GROUPS[group][1]

            def passes(acc, s, words_sb, scales_sb):
                for g in range(X_PASSES):
                    nc.tensor.matmul_mx(
                        out=acc,
                        lhsT=x_codes[group][:, s, g, :].bitcast(FP8X4),
                        lhsT_scale=x_scales[group][:, s, g, :],
                        rhs=words_sb[:, g, :].bitcast(FP8X4),
                        rhs_scale=scales_sb[:, g, :],
                        start=(g == 0),
                        stop=(g == X_PASSES - 1),
                    )

            long_acc = []
            for s in range(count):
                acc1 = psum.tile([P, HIDDEN], F32, tag="bank")
                passes(acc1[:], s, w1_words, w1_scales)
                long_acc.append(acc1)
            acc2 = psum.tile([P, count, HIDDEN2], F32, tag="bank")
            for s in range(count):
                passes(acc2[:, s, :], s, w2_words, w2_scales)
            sorted_h = work.tile([P, count, HIDDEN], BF16, tag="h_sorted")
            short = work.tile([P, count, HIDDEN2], BF16, tag="short")

            for s in range(count):
                nc.vector.scalar_tensor_tensor(
                    out=sorted_h[:, s, :], in0=long_acc[s][:],
                    scalar=push1[group][:, s : s + 1], in1=b1_sorted[:],
                    op0=ALU.add, op1=ALU.add,
                )
            for s in range(count):
                nc.vector.scalar_tensor_tensor(
                    out=short[:, s, :], in0=acc2[:, s, :],
                    scalar=push2[group][:, s : s + 1], in1=b2_sorted[:],
                    op0=ALU.add, op1=ALU.add,
                )
            h_sorted[group], h_short[group] = sorted_h, short

        def merge_branches(group):
            low = h_sorted[group][:].rearrange("r s (u n) -> r (s u) n", u=2)[:, :, 0 : 2 * P2]
            nc.vector.tensor_tensor(
                out=low, in0=low, in1=h_short[group][:].rearrange("r s (u n) -> r (s u) n", u=2), op=ALU.max
            )
            if GROUPS[group][1] == 2:
                whole = h_sorted[group][:].rearrange("r s n -> r (s n)")
                nc.gpsimd.tensor_scalar(out=whole, in0=whole, scalar1=FAR, scalar2=0.0, op0=ALU.min, op1=ALU.max)

        def transpose_h(group):
            count = GROUPS[group][1]
            ht = psum.tile([P, count, 2, P], F32, tag="bank")
            for s in range(count):
                words = h_sorted[group][:, s, :].bitcast(F32)
                for u in range(2):
                    nc.tensor.transpose(ht[:, s, u, :], words[:, P * u : P * (u + 1)], ident_f32[:])
            grouped = work.tile([P, count, P, PACK], BF16, tag="h_grouped", align_bytes=64)
            if count == 2:
                nc.scalar.copy(
                    out=grouped[:].rearrange("p s r t -> p s (r t)").bitcast(F32).rearrange("p s (r u) -> p s r u", u=2),
                    in_=ht[:].rearrange("p s u r -> p s r u"),
                )
            else:
                nc.scalar.activation(
                    out=grouped[:, 0].rearrange("p r (u e) -> p r u e", e=2),
                    in_=ht[:, 0].bitcast(BF16).rearrange("p u (r e) -> p r u e", e=2),
                    func=ACT.Relu,
                )
            h_grouped[group] = grouped

        def quantise_h(group):
            count = GROUPS[group][1]
            codes = work.tile([P, count, P], U32, tag="h_codes", align_bytes=64)
            scales = work.tile([P, count, P], U8, tag="h_scales", align_bytes=64)
            nc.vector.quantize_mx(
                out=codes[:].rearrange("p s r -> p (s r)").bitcast(FP8X4),
                scales=scales[:].rearrange("p s r -> p (s r)"),
                in_=h_grouped[group][:].rearrange("p s r t -> p (s r t)"),
            )
            h_codes[group], h_scales[group] = codes, scales

        def last_layer(group):
            first_tile, count = GROUPS[group]
            for s in range(count):
                result = work.tile([P, OUT], F32, tag="result", bufs=4)
                for first_col in range(0, OUT, BANK):
                    cols = slice(first_col, first_col + BANK)
                    acc = psum.tile([P, BANK], F32, tag="bank")
                    nc.tensor.matmul_mx(
                        out=acc[:],
                        lhsT=h_codes[group][:, s, :].bitcast(FP8X4),
                        lhsT_scale=h_scales[group][:, s, :],
                        rhs=wf_words[:, 0, cols].bitcast(FP8X4),
                        rhs_scale=wf_scales[:, 0, cols],
                        start=True,
                        stop=True,
                    )
                    if group < LAST_PAIR and s == 0 and first_col == BANK:
                        nc.scalar.copy(out=result[:, cols], in_=acc[:])
                        nc.gpsimd.tensor_tensor(
                            out=result[:, cols], in0=result[:, cols], in1=bf_all[:, cols], op=ALU.add
                        )
                    else:
                        nc.vector.tensor_tensor(out=result[:, cols], in0=acc[:], in1=bf_all[:, cols], op=ALU.add)
                    nc.sync.dma_start(out=out_rows[:, first_tile + s, cols], in_=result[:, cols])

        def in_range(group):
            return 0 <= group < N_GROUPS

        sort_scales(w1_scales, w1_scales_raw)
        keep_busy(4)
        for j in range(N_GROUPS + 3):
            if in_range(j):
                transpose_x(j)
                if j == 0:
                    keep_busy(3)
                tiles = range(GROUPS[j][1])
                early = 1 if j == 1 else len(tiles)
                sum_magnitudes(j, tiles[:early])
                copy_x(j)
                sum_magnitudes(j, tiles[early:])
            if in_range(j - 1):
                first_layer(j - 1)
            if in_range(j - 2):
                transpose_h(j - 2)
            if in_range(j):
                quantise_x(j)
                make_pushes(j)
            if in_range(j - 1):
                merge_branches(j - 1)
            if j == 0:
                sort_words(w1_words, w1_words_raw)
                spread_first_biases()
                sort_words(w2_words, w2_words_raw)
                sort_scales(w2_scales, w2_scales_raw)
            if j in (1, 2):
                spread_last_bias(j - 1)
            if in_range(j - 2):
                quantise_h(j - 2)
            if in_range(j - 3):
                last_layer(j - 3)
